import numpy as np
import ml_dtypes


BF16 = ml_dtypes.bfloat16


def bf(x):
    return np.asarray(x, np.float32).astype(BF16)


def f64(x):
    return np.asarray(x).astype(np.float64)


E2M1 = np.array([0.0, 0.5, 1.0, 1.5, 2.0, 3.0, 4.0, 6.0, -0.0, -0.5, -1.0, -1.5, -2.0, -3.0, -4.0, -6.0])


def pack_weight(w, fmt):
    k, n = w.shape
    w = f64(bf(w)).reshape(k // 32, 32, n)
    amax = np.abs(w).max(1)
    if fmt == "e4m3":
        byte = np.frexp(amax)[1] - 1 + 127 - 7
    else:
        mant, ex = np.frexp(amax / 6.0)
        byte = np.where(mant > 0.5, ex, ex - 1) + 127
    byte = np.clip(np.where(amax > 0, byte, 1), 1, 254)
    scaled = (w * np.exp2(127.0 - byte)[:, None, :]).reshape(k, n).astype(np.float32)
    by_word = np.ascontiguousarray(scaled.reshape(k // 512, 128, 4, n).transpose(0, 1, 3, 2))
    if fmt == "e4m3":
        words = by_word.astype(ml_dtypes.float8_e4m3fn).view(np.uint8)
    else:
        c = by_word.astype(ml_dtypes.float4_e2m1fn).view(np.uint8) & 0xF
        words = c[..., 0::2] | (c[..., 1::2] << 4)
    return np.ascontiguousarray(words), np.ascontiguousarray(byte.astype(np.uint8).reshape(k // 512, 16, n))


def unpack_weight(words, scales, fmt):
    g, p, n, _ = words.shape
    if fmt == "e4m3":
        vals = np.ascontiguousarray(words).view(ml_dtypes.float8_e4m3fn).astype(np.float64)
    else:
        nib = np.empty((g, p, n, 4), np.uint8)
        nib[..., 0::2] = words & 0xF
        nib[..., 1::2] = words >> 4
        vals = E2M1[nib]
    vals = vals * np.repeat(np.exp2(scales.astype(np.float64) - 127.0), 8, axis=1)[..., None]
    return vals.transpose(0, 1, 3, 2).reshape(g * 512, n)

def pack4(w):
    words, scales = pack_weight(w, "e2m1")
    return words.reshape(words.shape[0], 128, -1), scales


def unpack4(words, scales):
    return unpack_weight(words.reshape(words.shape[0], 128, -1, 2), scales, "e2m1")


def kspread(k):
    return np.exp2(np.repeat(np.random.randint(-6, 7, k // 32), 32).astype(np.float64))


B, L, D, H, HD, MINI, NCH, TEXT, OFF = 2, 256, 4096, 16, 256, 64, 4, 64, 128


def rope_table():
    inv_freq = 1.0 / (10000.0 ** (np.arange(0, HD, 2) / HD))
    ang = np.outer(np.arange(L), inv_freq)
    return np.stack([np.cos(ang), np.sin(ang)], axis=-1)


def l2norm(x):
    return x / np.maximum(np.sqrt((x * x).sum(-1, keepdims=True)), 1e-12)


def rope(x, cos, sin):
    c = cos[None, :, None, :]
    s = sin[None, :, None, :]
    xr, xi = x[..., 0::2], x[..., 1::2]
    return np.stack([xr * c - xi * s, xr * s + xi * c], axis=-1).reshape(x.shape)


def setup_inputs():
    s = kspread(D)
    hidden_states = np.random.standard_normal((B, L, D)) * s
    hidden_states_words, hidden_states_scales = pack4(hidden_states.reshape(B * L, D).T)
    freqs_cis = bf(rope_table())
    wk_w_words, wk_w_scales = pack4(np.random.standard_normal((D, D)) / np.sqrt(D) / s[:, None])
    wk_b = bf(np.random.standard_normal(D) * 0.1)
    wv_w_words, wv_w_scales = pack4(np.random.standard_normal((D, D)) * 0.5 / np.sqrt(D) / s[:, None])
    wv_b = bf(np.random.standard_normal(D) * 0.1)
    ttt_norm_weight = bf(1.0 + 0.1 * np.random.standard_normal((H, HD)))
    ttt_norm_bias = bf(0.1 * np.random.standard_normal((H, HD)))
    return {"hidden_states_words": hidden_states_words,
            "hidden_states_scales": hidden_states_scales,
            "freqs_cis": freqs_cis,
            "wk_w_words": wk_w_words,
            "wk_w_scales": wk_w_scales,
            "wk_b": wk_b,
            "wv_w_words": wv_w_words,
            "wv_w_scales": wv_w_scales,
            "wv_b": wv_b,
            "ttt_norm_weight": ttt_norm_weight,
            "ttt_norm_bias": ttt_norm_bias}


def reference(hidden_states_words, hidden_states_scales, freqs_cis, wk_w_words, wk_w_scales, wk_b, wv_w_words, wv_w_scales, wv_b, ttt_norm_weight, ttt_norm_bias):
    hq = unpack4(hidden_states_words, hidden_states_scales).T.reshape(B, L, D)
    xk = ((hq @ unpack4(wk_w_words, wk_w_scales)) + f64(wk_b)).reshape(B, L, H, HD)
    xv = ((hq @ unpack4(wv_w_words, wv_w_scales)) + f64(wv_b)).reshape(B, L, H, HD)
    fc = f64(freqs_cis)
    xk = rope(l2norm(xk), fc[..., 0], fc[..., 1])
    diff = xv - xk
    mean = diff.mean(axis=-1, keepdims=True)
    std = diff.std(axis=-1, keepdims=True, ddof=1)
    norm = (diff - mean) / (std + 1e-8)
    xv = f64(ttt_norm_weight)[None, None] * norm + f64(ttt_norm_bias)[None, None] + xk
    return xk, xv

@@ -1,0 +1,431 @@
+from contextlib import ExitStack
+
+import concourse.mybir as mybir
+from concourse.masks import make_identity
+
+F32 = mybir.dt.float32
+BF16 = mybir.dt.bfloat16
+U8 = mybir.dt.uint8
+I32 = mybir.dt.int32
+FP4 = mybir.dt.float4_e2m1fn_x4
+ACT = mybir.ActivationFunctionType
+ALU = mybir.AluOpType
+
+FLOPS = 2 * 512 * 4096 * 8192
+
+P = 128
+G = 8
+NCH = 8
+NSUB = 16
+WBUF = 3
+G_D2 = True
+G_F2 = True
+NWARM1 = 12
+NWARM2 = 6
+
+E24 = 0
+NE24 = 1
+E30 = 2
+E8 = 3
+
+
+def tile_tttwrapper_pa_kernel(
+    tc,
+    hidden_states_words,
+    hidden_states_scales,
+    freqs_cis,
+    wk_w_words,
+    wk_w_scales,
+    wk_b,
+    wv_w_words,
+    wv_w_scales,
+    wv_b,
+    ttt_norm_weight,
+    ttt_norm_bias,
+    out_0,
+    out_1,
+):
+    nc = tc.nc
+    o0 = out_0.rearrange("b l h d -> (b l) (h d)")
+    o1 = out_1.rearrange("b l h d -> (b l) (h d)")
+    wflat = ttt_norm_weight.rearrange("h d -> (h d)")
+    bflat = ttt_norm_bias.rearrange("h d -> (h d)")
+
+    with ExitStack() as ctx:
+        ctx.enter_context(tc.manual_schedule())
+        const = ctx.enter_context(tc.tile_pool(name="const", bufs=1))
+        wpool = ctx.enter_context(tc.tile_pool(name="wpool", bufs=WBUF))
+        work = ctx.enter_context(tc.tile_pool(name="work", bufs=2))
+        small = ctx.enter_context(tc.tile_pool(name="small", bufs=3))
+        psum = ctx.enter_context(tc.psum_pool(name="psum", bufs=3))
+
+        hc = const.tile([P, G, 1024], U8, name="hc", tag="hc", align_bytes=64)
+        hs = const.tile([P, G, 512], U8, name="hs", tag="hs", align_bytes=64)
+        ksc = []
+        vsc = []
+        for r in range(WBUF):
+            ks_t = const.tile([P, G, 512], U8, name="ksc%d" % r, tag="ksc%d" % r, align_bytes=64)
+            vs_t = const.tile([P, G, 512], U8, name="vsc%d" % r, tag="vsc%d" % r, align_bytes=64)
+            ksc.append(ks_t)
+            vsc.append(vs_t)
+        bk = const.tile([P, 4096], BF16, name="bk", tag="bk")
+        bv = const.tile([P, 4096], BF16, name="bv", tag="bv")
+        wt = const.tile([P, 4096], BF16, name="wt", tag="wt")
+        bt = const.tile([P, 4096], BF16, name="bt", tag="bt")
+        fc = const.tile([P, 512], BF16, name="fc", tag="fc")
+        fc2 = const.tile([P, 512], BF16, name="fc2", tag="fc2")
+        eps = const.tile([P, 4], F32, name="eps", tag="eps")
+        scr = const.tile([P, 1], F32, name="scr", tag="scr")
+        wz = const.tile([P, 512], BF16, name="wz", tag="wz")
+        ident = const.tile([P, P], BF16, name="ident", tag="ident")
+        fcp = psum.tile([P, 512], F32, name="fcp", tag="fcp", bufs=1)
+        fc2p = psum.tile([P, 512], F32, name="fc2p", tag="fc2p", bufs=1)
+
+        def load_scales(planes, src, cols, qs=(0, 1, 2, 3)):
+            for q in qs:
+                nc.sync.dma_start(
+                    out=planes[32 * q : 32 * q + 4, :, :].bitcast(I32),
+                    in_=src[:, 4 * q : 4 * q + 4, cols].rearrange("g r n -> r g n").bitcast(I32),
+                )
+
+        def load_codes(dst, src, cols, g0=0, g1=G):
+            nc.sync.dma_start(
+                out=dst[:, g0:g1, :].bitcast(I32),
+                in_=src[g0:g1, :, cols].rearrange("g p n -> p g n").bitcast(I32),
+            )
+
+        def load_table(dst, src, lo, hi):
+            nc.sync.dma_start(out=dst[:, lo:hi], in_=src[lo:hi].partition_broadcast(P))
+
+        wcodes = {}
+
+        def alloc_codes(c):
+            kc = wpool.tile([P, G, 1024], U8, name="kc%d" % c, tag="kc", align_bytes=64)
+            vc = wpool.tile([P, G, 1024], U8, name="vc%d" % c, tag="vc", align_bytes=64)
+            wcodes[c] = (kc, vc)
+            return kc, vc
+
+        def load_chunk(c):
+            kc, vc = alloc_codes(c)
+            load_scales(ksc[c % WBUF], wk_w_scales, slice(512 * c, 512 * c + 512))
+            load_scales(vsc[c % WBUF], wv_w_scales, slice(512 * c, 512 * c + 512))
+            load_codes(kc, wk_w_words, slice(1024 * c, 1024 * c + 1024))
+            load_codes(vc, wv_w_words, slice(1024 * c, 1024 * c + 1024))
+
+        make_identity(nc, ident[:])
+        nc.vector.memset(wz[:], 0.0)
+        nc.vector.memset(hs[:].bitcast(I32), 0)
+        nc.vector.memset(ksc[0][:].bitcast(I32), 0)
+        nc.vector.memset(eps[:, E24 : E24 + 1], 1e-24)
+        nc.vector.memset(eps[:, NE24 : NE24 + 1], -1e-24)
+        nc.vector.memset(eps[:, E30 : E30 + 1], 1e-30)
+        nc.vector.memset(eps[:, E8 : E8 + 1], 1e-8)
+        nc.vector.memset(vsc[0][:].bitcast(I32), 0)
+        nc.vector.memset(ksc[1][:].bitcast(I32), 0)
+        nc.vector.memset(vsc[1][:].bitcast(I32), 0)
+        nc.scalar.activation(out=scr[:], in_=eps[:, E8 : E8 + 1], func=ACT.Sqrt)
+
+        kc0, vc0 = alloc_codes(0)
+        hb0 = hc[:, :, 0:512]
+        hb1 = hc[:, :, 512:1024]
+        nc.sync.dma_start(
+            out=fc[:].rearrange("p (t n) -> p t n", t=2), in_=freqs_cis.rearrange("(t p) j e -> p t (j e)", p=P)
+        )
+        load_scales(hs, hidden_states_scales, slice(0, 512), (0, 1, 2))
+        load_codes(hb0, hidden_states_words, slice(0, 512))
+        load_codes(kc0, wk_w_words, slice(0, 1024), 0, 4)
+        load_scales(hs, hidden_states_scales, slice(0, 512), (3,))
+        load_scales(ksc[0], wk_w_scales, slice(0, 512))
+        load_codes(kc0, wk_w_words, slice(0, 1024), 4, 8)
+        load_table(bk, wk_b, 0, 512)
+        load_scales(vsc[0], wv_w_scales, slice(0, 512))
+        load_codes(vc0, wv_w_words, slice(0, 1024))
+        load_table(bv, wv_b, 0, 512)
+        load_codes(hb1, hidden_states_words, slice(512, 1024))
+        load_table(bt, bflat, 0, 512)
+        load_table(wt, wflat, 0, 512)
+        load_chunk(1)
+        load_table(bk, wk_b, 512, 4096)
+        load_table(bv, wv_b, 512, 4096)
+        load_table(bt, bflat, 512, 4096)
+        load_table(wt, wflat, 512, 4096)
+
+        fcv = fc[:].rearrange("p (n e) -> p n e", e=2)
+        fc2v = fc2[:].rearrange("p (n e) -> p n e", e=2)
+        nc.vector.tensor_scalar_mul(out=fc2v[:, :, 0:1], in0=fcv[:, :, 1:2], scalar1=-1.0)
+        nc.vector.tensor_copy(out=fc2v[:, :, 1:2], in_=fcv[:, :, 0:1])
+        nc.vector.memset(ksc[2][:].bitcast(I32), 0)
+        nc.vector.memset(vsc[2][:].bitcast(I32), 0)
+        load_chunk(2)
+
+        warm = psum.tile([P, 512], F32, name="warm", tag="pk", bufs=3)
+        for r in range(NWARM1):
+            nc.tensor.matmul(out=warm[:], lhsT=wz[:, 0:128], rhs=wz[:], start=True, stop=True)
+        nc.tensor.matmul(out=fcp[:], lhsT=ident[:], rhs=fc[:], start=True, stop=True)
+        nc.tensor.matmul(out=fc2p[:], lhsT=ident[:], rhs=fc2[:], start=True, stop=True)
+        for r in range(NWARM2):
+            nc.tensor.matmul(out=warm[:], lhsT=wz[:, 0:128], rhs=wz[:], start=True, stop=True)
+
+        SH4 = [P, 2, 128, 2]
+
+        def v4(ap):
+            return ap.rearrange("p (h j e) -> p h j e", h=2, j=128, e=2)
+
+        def tab(ps, t):
+            return ps[:, 256 * t : 256 * t + 256].rearrange("p (j e) -> p j e", e=2).unsqueeze(1).to_broadcast(SH4)
+
+        st = {}
+
+        def pe(s, kind):
+            c, b = divmod(s, 2)
+            codes = wcodes[c][0 if kind == "pk" else 1]
+            planes = (ksc if kind == "pk" else vsc)[c % WBUF]
+            res = []
+            for t in range(2):
+                m = 2 * b + t
+                acc = psum.tile([P, 512], F32, name="%s_%d_%d" % (kind, s, t), tag=kind, bufs=3)
+                for g in range(G):
+                    nc.tensor.matmul_mx(
+                        out=acc[:],
+                        lhsT=hc[:, g, 256 * m : 256 * m + 256].bitcast(FP4),
+                        lhsT_scale=hs[:, g, 128 * m : 128 * m + 128],
+                        rhs=codes[:, g, :].bitcast(FP4),
+                        rhs_scale=planes[:, g, :],
+                        start=(g == 0),
+                        stop=(g == G - 1),
+                    )
+                res.append(acc)
+            if s not in st:
+                st[s] = {}
+            st[s][kind] = res
+
+        def cols(s):
+            c = s // 2
+            return slice(512 * c, 512 * c + 512)
+
+        def rows(s, t):
+            r0 = 256 * (s % 2) + 128 * t
+            return slice(r0, r0 + 128)
+
+        def rows2(s):
+            b = s % 2
+            return slice(256 * b, 256 * b + 256)
+
+        def wtile(s, nm, bufs, tag=None):
+            tl = work.tile([P, 2, 512], F32, name="%s%d" % (nm, s), tag=(tag or nm), bufs=bufs)
+            st[s][nm] = tl
+            return tl
+
+        def stile(s, nm):
+            tl = small.tile([P, 4], F32, name="%s%d" % (nm, s), tag=nm, bufs=3)
+            st[s][nm] = tl
+            return tl
+
+        def junk():
+            return work.tile([P, 256], F32, name="junk", tag="junk", bufs=4)
+
+        def hsl(h):
+            return slice(256 * h, 256 * h + 256)
+
+        def col(tl, k):
+            return tl[:, k : k + 1]
+
+        def a1(s):
+            k0 = wtile(s, "k0", 2)
+            for t in range(2):
+                nc.vector.tensor_tensor(out=k0[:, t, :], in0=st[s]["pk"][t][:], in1=bk[:, cols(s)], op=ALU.add)
+
+        def a2(s):
+            pp = wtile(s, "pp", 4)
+            for t in range(2):
+                nc.vector.tensor_tensor(out=pp[:, t, :], in0=st[s]["pv"][t][:], in1=bv[:, cols(s)], op=ALU.add)
+
+        def c1(s, k):
+            t, h = divmod(k, 2)
+            jk = junk()
+            nc.scalar.activation(
+                out=jk[:], in_=st[s]["k0"][:, t, hsl(h)], func=ACT.Square, accum_out=col(st[s]["ss"], k)
+            )
+
+        def b1(s, t):
+            nc.vector.tensor_tensor(
+                out=v4(st[s]["t1"][:, t, :]),
+                in0=v4(st[s]["k0"][:, t, :])[:, :, :, 0:1].to_broadcast(SH4),
+                in1=tab(fcp, t),
+                op=ALU.mult,
+            )
+
+        def b2(s, t):
+            nc.vector.tensor_tensor(
+                out=v4(st[s]["t2"][:, t, :]),
+                in0=v4(st[s]["k0"][:, t, :])[:, :, :, 1:2].to_broadcast(SH4),
+                in1=tab(fc2p, t),
+                op=ALU.mult,
+            )
+
+        def b3(s, t):
+            t1 = st[s]["t1"]
+            nc.vector.tensor_tensor(out=t1[:, t, :], in0=t1[:, t, :], in1=st[s]["t2"][:, t, :], op=ALU.add)
+
+        def c2(s):
+            xk = wtile(s, "xk", 3)
+            t1 = st[s]["t1"]
+            rn = st[s]["rno"]
+            for k in range(4):
+                t, h = divmod(k, 2)
+                nc.scalar.activation(out=xk[:, t, hsl(h)], in_=t1[:, t, hsl(h)], func=ACT.Copy, scale=col(rn, k))
+            nc.sync.dma_start(out=o0[rows2(s), cols(s)].rearrange("(t p) n -> p t n", p=P), in_=xk[:])
+
+        def d1(s, t):
+            pp = st[s]["pp"]
+            nc.vector.tensor_tensor(out=pp[:, t, :], in0=pp[:, t, :], in1=st[s]["xk"][:, t, :], op=ALU.subtract)
+
+        def d2(s, t, tag, bufs):
+            xb = work.tile([P, 512], F32, name="xb%d_%d" % (t, s), tag=tag, bufs=bufs)
+            st[s]["xb%d" % t] = xb
+            eng = nc.gpsimd if G_D2 else nc.vector
+            eng.tensor_tensor(out=xb[:], in0=st[s]["xk"][:, t, :], in1=bt[:, cols(s)], op=ALU.add)
+
+        def e1(s, k):
+            t, h = divmod(k, 2)
+            jk = junk()
+            nc.scalar.activation(
+                out=jk[:],
+                in_=st[s]["pp"][:, t, hsl(h)],
+                func=ACT.Identity,
+                scale=-1.0 / 256.0,
+                accum_out=col(st[s]["negm"], k),
+            )
+
+        def e2(s, k):
+            t, h = divmod(k, 2)
+            jk = junk()
+            nc.scalar.activation(
+                out=jk[:],
+                in_=st[s]["pp"][:, t, hsl(h)],
+                func=ACT.Square,
+                bias=col(st[s]["negm"], k),
+                scale=1.0,
+                accum_out=col(st[s]["ssd"], k),
+            )
+
+        def nmul(s):
+            nma = stile(s, "nma")
+            for k in range(4):
+                nc.scalar.activation(
+                    out=col(nma, k), in_=col(st[s]["negm"], k), func=ACT.Copy, scale=col(st[s]["rao"], k)
+                )
+
+        def e3(s):
+            pp = st[s]["pp"]
+            for k in range(4):
+                t, h = divmod(k, 2)
+                nc.scalar.activation(
+                    out=pp[:, t, hsl(h)],
+                    in_=pp[:, t, hsl(h)],
+                    func=ACT.Identity,
+                    bias=col(st[s]["nma"], k),
+                    scale=col(st[s]["rao"], k),
+                )
+
+        def f1(s, t):
+            pp = st[s]["pp"]
+            nc.vector.tensor_tensor(out=pp[:, t, :], in0=pp[:, t, :], in1=wt[:, cols(s)], op=ALU.mult)
+
+        def f2(s, t, on_g):
+            pp = st[s]["pp"]
+            eng = nc.gpsimd if on_g else nc.vector
+            eng.tensor_tensor(out=pp[:, t, :], in0=pp[:, t, :], in1=st[s]["xb%d" % t][:], op=ALU.add)
+
+        def store_xv(s):
+            nc.sync.dma_start(out=o1[rows2(s), cols(s)].rearrange("(t p) n -> p t n", p=P), in_=st[s]["pp"][:])
+
+        def store_xv_half(s, t):
+            nc.sync.dma_start(out=o1[rows(s, t), cols(s)], in_=st[s]["pp"][:, t, :])
+
+        def sqrt_e(s):
+            sdv = stile(s, "sdv")
+            nc.scalar.activation(
+                out=sdv[:], in_=st[s]["ssd"][:], func=ACT.Sqrt, bias=col(eps, E30), scale=1.0 / 255.0
+            )
+
+        def add_e(s):
+            rca = stile(s, "rca")
+            nc.scalar.activation(out=rca[:], in_=st[s]["sdv"][:], func=ACT.Identity, bias=col(eps, E8), scale=1.0)
+
+        pe(0, "pk")
+        pe(0, "pv")
+        for i in range(NSUB + 1):
+            cur = i < NSUB
+            prev = i >= 1
+            j = i - 1
+            if i % 2 == 1 and (i // 2) + 3 < NCH:
+                load_chunk((i // 2) + 3)
+            if cur:
+                a1(i)
+                if i + 1 < NSUB:
+                    pe(i + 1, "pk")
+                stile(i, "ss")
+                c1(i, 0)
+            if prev:
+                sqrt_e(j)
+            if cur:
+                c1(i, 1)
+            if prev:
+                add_e(j)
+            if cur:
+                c1(i, 2)
+                c1(i, 3)
+                r1 = stile(i, "r1")
+                nc.scalar.activation(out=r1[:], in_=st[i]["ss"][:], func=ACT.Relu, bias=col(eps, NE24), scale=1.0)
+                rcn = stile(i, "rcn")
+                nc.scalar.activation(out=rcn[:], in_=r1[:], func=ACT.Sqrt, bias=col(eps, E24), scale=1.0)
+                wtile(i, "t1", 2)
+                wtile(i, "t2", 1, tag="t2%d" % (i % 2))
+                b1(i, 0)
+                b2(i, 0)
+                b1(i, 1)
+            if prev:
+                rao = stile(j, "rao")
+                nc.vector.reciprocal(out=rao[:], in_=st[j]["rca"][:])
+            if cur:
+                b2(i, 1)
+            if prev:
+                nmul(j)
+                e3(j)
+            if cur:
+                b3(i, 0)
+                rno = stile(i, "rno")
+                nc.vector.reciprocal(out=rno[:], in_=st[i]["rcn"][:])
+                b3(i, 1)
+                c2(i)
+                a2(i)
+                if i + 1 < NSUB:
+                    pe(i + 1, "pv")
+            if prev:
+                d2(j, 1, "t2%d" % (i % 2), 1)
+            if cur:
+                d1(i, 0)
+                d1(i, 1)
+            if prev:
+                if cur:
+                    f1(j, 0)
+                    f1(j, 1)
+                    f2(j, 0, G_F2)
+                    f2(j, 1, G_F2)
+                    store_xv(j)
+                else:
+                    f1(j, 0)
+                    f1(j, 1)
+                    f2(j, 0, False)
+                    store_xv_half(j, 0)
+                    f2(j, 1, False)
+                    store_xv_half(j, 1)
+            if cur:
+                d2(i, 0, "xw", 2)
+                stile(i, "negm")
+                stile(i, "ssd")
+                for k in range(4):
+                    e1(i, k)
+                for k in range(4):
+                    e2(i, k)

@@ -18,10 +18,7 @@ G = 8
 NCH = 8
 NSUB = 16
 WBUF = 3
-G_D2 = True
-G_F2 = True
-NWARM1 = 12
-NWARM2 = 6
+USE_G = True
 
 E24 = 0
 NE24 = 1
@@ -57,9 +54,12 @@ def tile_tttwrapper_pa_kernel(
         wpool = ctx.enter_context(tc.tile_pool(name="wpool", bufs=WBUF))
         work = ctx.enter_context(tc.tile_pool(name="work", bufs=2))
         small = ctx.enter_context(tc.tile_pool(name="small", bufs=3))
-        psum = ctx.enter_context(tc.psum_pool(name="psum", bufs=3))
+        psum = ctx.enter_context(tc.psum_pool(name="psum", bufs=2))
 
-        hc = const.tile([P, G, 1024], U8, name="hc", tag="hc", align_bytes=64)
+        hcb = []
+        for r in range(2):
+            hc_t = const.tile([P, G, 512], U8, name="hc%d" % r, tag="hc%d" % r, align_bytes=64)
+            hcb.append(hc_t)
         hs = const.tile([P, G, 512], U8, name="hs", tag="hs", align_bytes=64)
         ksc = []
         vsc = []
@@ -70,29 +70,25 @@ def tile_tttwrapper_pa_kernel(
             vsc.append(vs_t)
         bk = const.tile([P, 4096], BF16, name="bk", tag="bk")
         bv = const.tile([P, 4096], BF16, name="bv", tag="bv")
-        wt = const.tile([P, 4096], BF16, name="wt", tag="wt")
         bt = const.tile([P, 4096], BF16, name="bt", tag="bt")
+        wrow = const.tile([P, 4096], BF16, name="wrow", tag="wrow")
         fc = const.tile([P, 512], BF16, name="fc", tag="fc")
         fc2 = const.tile([P, 512], BF16, name="fc2", tag="fc2")
         eps = const.tile([P, 4], F32, name="eps", tag="eps")
         scr = const.tile([P, 1], F32, name="scr", tag="scr")
-        wz = const.tile([P, 512], BF16, name="wz", tag="wz")
+        ones = const.tile([P, P], BF16, name="ones", tag="ones")
         ident = const.tile([P, P], BF16, name="ident", tag="ident")
-        fcp = psum.tile([P, 512], F32, name="fcp", tag="fcp", bufs=1)
-        fc2p = psum.tile([P, 512], F32, name="fc2p", tag="fc2p", bufs=1)
+        tbl = psum.tile([P, 1024], BF16, name="tbl", tag="tbl", bufs=1)
 
-        def load_scales(planes, src, cols, qs=(0, 1, 2, 3)):
-            for q in qs:
+        def load_scales(planes, src, cols):
+            for q in range(4):
                 nc.sync.dma_start(
                     out=planes[32 * q : 32 * q + 4, :, :].bitcast(I32),
                     in_=src[:, 4 * q : 4 * q + 4, cols].rearrange("g r n -> r g n").bitcast(I32),
                 )
 
-        def load_codes(dst, src, cols, g0=0, g1=G):
-            nc.sync.dma_start(
-                out=dst[:, g0:g1, :].bitcast(I32),
-                in_=src[g0:g1, :, cols].rearrange("g p n -> p g n").bitcast(I32),
-            )
+        def load_codes(dst, src, cols):
+            nc.sync.dma_start(out=dst[:].bitcast(I32), in_=src[:, :, cols].rearrange("g p n -> p g n").bitcast(I32))
 
         def load_table(dst, src, lo, hi):
             nc.sync.dma_start(out=dst[:, lo:hi], in_=src[lo:hi].partition_broadcast(P))
@@ -112,10 +108,11 @@ def tile_tttwrapper_pa_kernel(
             load_codes(kc, wk_w_words, slice(1024 * c, 1024 * c + 1024))
             load_codes(vc, wv_w_words, slice(1024 * c, 1024 * c + 1024))
 
+        nc.gpsimd.memset(wrow[:].bitcast(F32), 0.0)
         make_identity(nc, ident[:])
-        nc.vector.memset(wz[:], 0.0)
         nc.vector.memset(hs[:].bitcast(I32), 0)
         nc.vector.memset(ksc[0][:].bitcast(I32), 0)
+        nc.vector.memset(ones[:], 1.0)
         nc.vector.memset(eps[:, E24 : E24 + 1], 1e-24)
         nc.vector.memset(eps[:, NE24 : NE24 + 1], -1e-24)
         nc.vector.memset(eps[:, E30 : E30 + 1], 1e-30)
@@ -126,29 +123,24 @@ def tile_tttwrapper_pa_kernel(
         nc.scalar.activation(out=scr[:], in_=eps[:, E8 : E8 + 1], func=ACT.Sqrt)
 
         kc0, vc0 = alloc_codes(0)
-        hb0 = hc[:, :, 0:512]
-        hb1 = hc[:, :, 512:1024]
         nc.sync.dma_start(
             out=fc[:].rearrange("p (t n) -> p t n", t=2), in_=freqs_cis.rearrange("(t p) j e -> p t (j e)", p=P)
         )
-        load_scales(hs, hidden_states_scales, slice(0, 512), (0, 1, 2))
-        load_codes(hb0, hidden_states_words, slice(0, 512))
-        load_codes(kc0, wk_w_words, slice(0, 1024), 0, 4)
-        load_scales(hs, hidden_states_scales, slice(0, 512), (3,))
+        load_codes(hcb[0], hidden_states_words, slice(0, 512))
+        load_codes(kc0, wk_w_words, slice(0, 1024))
+        load_scales(hs, hidden_states_scales, slice(0, 512))
+        nc.sync.dma_start(out=wrow[0:1, :], in_=wflat.rearrange("(o n) -> o n", o=1))
         load_scales(ksc[0], wk_w_scales, slice(0, 512))
-        load_codes(kc0, wk_w_words, slice(0, 1024), 4, 8)
         load_table(bk, wk_b, 0, 512)
         load_scales(vsc[0], wv_w_scales, slice(0, 512))
         load_codes(vc0, wv_w_words, slice(0, 1024))
         load_table(bv, wv_b, 0, 512)
-        load_codes(hb1, hidden_states_words, slice(512, 1024))
+        load_codes(hcb[1], hidden_states_words, slice(512, 1024))
         load_table(bt, bflat, 0, 512)
-        load_table(wt, wflat, 0, 512)
         load_chunk(1)
         load_table(bk, wk_b, 512, 4096)
         load_table(bv, wv_b, 512, 4096)
         load_table(bt, bflat, 512, 4096)
-        load_table(wt, wflat, 512, 4096)
 
         fcv = fc[:].rearrange("p (n e) -> p n e", e=2)
         fc2v = fc2[:].rearrange("p (n e) -> p n e", e=2)
@@ -158,21 +150,36 @@ def tile_tttwrapper_pa_kernel(
         nc.vector.memset(vsc[2][:].bitcast(I32), 0)
         load_chunk(2)
 
-        warm = psum.tile([P, 512], F32, name="warm", tag="pk", bufs=3)
-        for r in range(NWARM1):
-            nc.tensor.matmul(out=warm[:], lhsT=wz[:, 0:128], rhs=wz[:], start=True, stop=True)
-        nc.tensor.matmul(out=fcp[:], lhsT=ident[:], rhs=fc[:], start=True, stop=True)
-        nc.tensor.matmul(out=fc2p[:], lhsT=ident[:], rhs=fc2[:], start=True, stop=True)
-        for r in range(NWARM2):
-            nc.tensor.matmul(out=warm[:], lhsT=wz[:, 0:128], rhs=wz[:], start=True, stop=True)
+        nc.tensor.matmul(out=tbl[:, 0:512], lhsT=ident[:], rhs=fc[:], start=True, stop=True)
+        nc.tensor.matmul(out=tbl[:, 512:1024], lhsT=ident[:], rhs=fc2[:], start=True, stop=True)
+
+        twt = {}
+
+        def put_w(pair):
+            tl = psum.tile([P, 1024], BF16, name="tw_%d" % pair, tag="tw%d" % (pair % 3), bufs=1)
+            for u in range(2):
+                c = 2 * pair + u
+                nc.tensor.matmul(
+                    out=tl[:, 512 * u : 512 * u + 512],
+                    lhsT=ones[:],
+                    rhs=wrow[:, 512 * c : 512 * c + 512],
+                    start=True,
+                    stop=True,
+                )
+                twt[c] = tl[:, 512 * u : 512 * u + 512]
+
+        put_w(0)
+        put_w(1)
+        put_w(2)
 
         SH4 = [P, 2, 128, 2]
+        SH3 = [P, 128, 2]
 
         def v4(ap):
             return ap.rearrange("p (h j e) -> p h j e", h=2, j=128, e=2)
 
-        def tab(ps, t):
-            return ps[:, 256 * t : 256 * t + 256].rearrange("p (j e) -> p j e", e=2).unsqueeze(1).to_broadcast(SH4)
+        def v3(ap):
+            return ap.rearrange("p (j e) -> p j e", e=2)
 
         st = {}
 
@@ -183,11 +190,11 @@ def tile_tttwrapper_pa_kernel(
             res = []
             for t in range(2):
                 m = 2 * b + t
-                acc = psum.tile([P, 512], F32, name="%s_%d_%d" % (kind, s, t), tag=kind, bufs=3)
+                acc = psum.tile([P, 512], F32, name="%s_%d_%d" % (kind, s, t), tag=kind, bufs=2)
                 for g in range(G):
                     nc.tensor.matmul_mx(
                         out=acc[:],
-                        lhsT=hc[:, g, 256 * m : 256 * m + 256].bitcast(FP4),
+                        lhsT=hcb[b][:, g, 256 * t : 256 * t + 256].bitcast(FP4),
                         lhsT_scale=hs[:, g, 128 * m : 128 * m + 128],
                         rhs=codes[:, g, :].bitcast(FP4),
                         rhs_scale=planes[:, g, :],
@@ -211,13 +218,13 @@ def tile_tttwrapper_pa_kernel(
             b = s % 2
             return slice(256 * b, 256 * b + 256)
 
-        def wtile(s, nm, bufs, tag=None):
-            tl = work.tile([P, 2, 512], F32, name="%s%d" % (nm, s), tag=(tag or nm), bufs=bufs)
+        def wtile(s, nm, bufs):
+            tl = work.tile([P, 2, 512], F32, name="%s%d" % (nm, s), tag=nm, bufs=bufs)
             st[s][nm] = tl
             return tl
 
         def stile(s, nm):
-            tl = small.tile([P, 4], F32, name="%s%d" % (nm, s), tag=nm, bufs=3)
+            tl = small.tile([P, 4], F32, name="%s%d" % (nm, s), tag=nm, bufs=4)
             st[s][nm] = tl
             return tl
 
@@ -230,15 +237,11 @@ def tile_tttwrapper_pa_kernel(
         def col(tl, k):
             return tl[:, k : k + 1]
 
-        def a1(s):
-            k0 = wtile(s, "k0", 2)
-            for t in range(2):
-                nc.vector.tensor_tensor(out=k0[:, t, :], in0=st[s]["pk"][t][:], in1=bk[:, cols(s)], op=ALU.add)
+        def a1(s, t):
+            nc.vector.tensor_tensor(out=st[s]["k0"][:, t, :], in0=st[s]["pk"][t][:], in1=bk[:, cols(s)], op=ALU.add)
 
-        def a2(s):
-            pp = wtile(s, "pp", 4)
-            for t in range(2):
-                nc.vector.tensor_tensor(out=pp[:, t, :], in0=st[s]["pv"][t][:], in1=bv[:, cols(s)], op=ALU.add)
+        def a2(s, t):
+            nc.vector.tensor_tensor(out=st[s]["pp"][:, t, :], in0=st[s]["pv"][t][:], in1=bv[:, cols(s)], op=ALU.add)
 
         def c1(s, k):
             t, h = divmod(k, 2)
@@ -251,39 +254,46 @@ def tile_tttwrapper_pa_kernel(
             nc.vector.tensor_tensor(
                 out=v4(st[s]["t1"][:, t, :]),
                 in0=v4(st[s]["k0"][:, t, :])[:, :, :, 0:1].to_broadcast(SH4),
-                in1=tab(fcp, t),
+                in1=v3(tbl[:, 256 * t : 256 * t + 256]).unsqueeze(1).to_broadcast(SH4),
                 op=ALU.mult,
             )
 
-        def b2(s, t):
-            nc.vector.tensor_tensor(
-                out=v4(st[s]["t2"][:, t, :]),
-                in0=v4(st[s]["k0"][:, t, :])[:, :, :, 1:2].to_broadcast(SH4),
-                in1=tab(fc2p, t),
-                op=ALU.mult,
+        def b2(s, k):
+            t, h = divmod(k, 2)
+            nc.vector.scalar_tensor_tensor(
+                out=v3(st[s]["t2"][:, t, hsl(h)]),
+                in0=v3(st[s]["k0"][:, t, hsl(h)])[:, :, 1:2].to_broadcast(SH3),
+                scalar=col(st[s]["rno"], k),
+                in1=v3(tbl[:, 512 + 256 * t : 512 + 256 * t + 256]),
+                op0=ALU.mult,
+                op1=ALU.mult,
             )
 
-        def b3(s, t):
-            t1 = st[s]["t1"]
-            nc.vector.tensor_tensor(out=t1[:, t, :], in0=t1[:, t, :], in1=st[s]["t2"][:, t, :], op=ALU.add)
+        def b3(s, k):
+            t, h = divmod(k, 2)
+            nc.vector.scalar_tensor_tensor(
+                out=st[s]["xk"][:, t, hsl(h)],
+                in0=st[s]["t1"][:, t, hsl(h)],
+                scalar=col(st[s]["rno"], k),
+                in1=st[s]["t2"][:, t, hsl(h)],
+                op0=ALU.mult,
+                op1=ALU.add,
+            )
 
-        def c2(s):
-            xk = wtile(s, "xk", 3)
-            t1 = st[s]["t1"]
-            rn = st[s]["rno"]
-            for k in range(4):
-                t, h = divmod(k, 2)
-                nc.scalar.activation(out=xk[:, t, hsl(h)], in_=t1[:, t, hsl(h)], func=ACT.Copy, scale=col(rn, k))
-            nc.sync.dma_start(out=o0[rows2(s), cols(s)].rearrange("(t p) n -> p t n", p=P), in_=xk[:])
+        def store_xk(s):
+            nc.sync.dma_start(out=o0[rows2(s), cols(s)].rearrange("(t p) n -> p t n", p=P), in_=st[s]["xk"][:])
 
         def d1(s, t):
             pp = st[s]["pp"]
             nc.vector.tensor_tensor(out=pp[:, t, :], in0=pp[:, t, :], in1=st[s]["xk"][:, t, :], op=ALU.subtract)
 
-        def d2(s, t, tag, bufs):
-            xb = work.tile([P, 512], F32, name="xb%d_%d" % (t, s), tag=tag, bufs=bufs)
+        def d2(s, t, on_g):
+            if t == 0:
+                xb = work.tile([P, 512], F32, name="xb0_%d" % s, tag="xa%d" % (s % 3), bufs=1)
+            else:
+                xb = work.tile([P, 512], F32, name="xb1_%d" % s, tag="xc", bufs=3)
             st[s]["xb%d" % t] = xb
-            eng = nc.gpsimd if G_D2 else nc.vector
+            eng = nc.gpsimd if on_g else nc.vector
             eng.tensor_tensor(out=xb[:], in0=st[s]["xk"][:, t, :], in1=bt[:, cols(s)], op=ALU.add)
 
         def e1(s, k):
@@ -309,28 +319,20 @@ def tile_tttwrapper_pa_kernel(
                 accum_out=col(st[s]["ssd"], k),
             )
 
-        def nmul(s):
-            nma = stile(s, "nma")
-            for k in range(4):
-                nc.scalar.activation(
-                    out=col(nma, k), in_=col(st[s]["negm"], k), func=ACT.Copy, scale=col(st[s]["rao"], k)
-                )
-
-        def e3(s):
+        def e3(s, k):
+            t, h = divmod(k, 2)
             pp = st[s]["pp"]
-            for k in range(4):
-                t, h = divmod(k, 2)
-                nc.scalar.activation(
-                    out=pp[:, t, hsl(h)],
-                    in_=pp[:, t, hsl(h)],
-                    func=ACT.Identity,
-                    bias=col(st[s]["nma"], k),
-                    scale=col(st[s]["rao"], k),
-                )
+            nc.scalar.activation(
+                out=pp[:, t, hsl(h)],
+                in_=pp[:, t, hsl(h)],
+                func=ACT.Identity,
+                bias=col(st[s]["nma"], k),
+                scale=col(st[s]["rao"], k),
+            )
 
         def f1(s, t):
             pp = st[s]["pp"]
-            nc.vector.tensor_tensor(out=pp[:, t, :], in0=pp[:, t, :], in1=wt[:, cols(s)], op=ALU.mult)
+            nc.vector.tensor_tensor(out=pp[:, t, :], in0=pp[:, t, :], in1=twt[s // 2], op=ALU.mult)
 
         def f2(s, t, on_g):
             pp = st[s]["pp"]
@@ -343,89 +345,88 @@ def tile_tttwrapper_pa_kernel(
         def store_xv_half(s, t):
             nc.sync.dma_start(out=o1[rows(s, t), cols(s)], in_=st[s]["pp"][:, t, :])
 
-        def sqrt_e(s):
-            sdv = stile(s, "sdv")
-            nc.scalar.activation(
-                out=sdv[:], in_=st[s]["ssd"][:], func=ACT.Sqrt, bias=col(eps, E30), scale=1.0 / 255.0
-            )
-
-        def add_e(s):
-            rca = stile(s, "rca")
-            nc.scalar.activation(out=rca[:], in_=st[s]["sdv"][:], func=ACT.Identity, bias=col(eps, E8), scale=1.0)
-
         pe(0, "pk")
         pe(0, "pv")
-        for i in range(NSUB + 1):
+        for i in range(NSUB + 2):
             cur = i < NSUB
-            prev = i >= 1
-            j = i - 1
+            p1 = 1 <= i <= NSUB
+            p2 = i >= 2
+            j1 = i - 1
+            j2 = i - 2
             if i % 2 == 1 and (i // 2) + 3 < NCH:
                 load_chunk((i // 2) + 3)
             if cur:
-                a1(i)
+                wtile(i, "k0", 2)
+                a1(i, 0)
+                a1(i, 1)
+                if i == 6:
+                    put_w(3)
                 if i + 1 < NSUB:
                     pe(i + 1, "pk")
                 stile(i, "ss")
-                c1(i, 0)
-            if prev:
-                sqrt_e(j)
-            if cur:
-                c1(i, 1)
-            if prev:
-                add_e(j)
-            if cur:
-                c1(i, 2)
-                c1(i, 3)
+                for k in range(4):
+                    c1(i, k)
                 r1 = stile(i, "r1")
                 nc.scalar.activation(out=r1[:], in_=st[i]["ss"][:], func=ACT.Relu, bias=col(eps, NE24), scale=1.0)
                 rcn = stile(i, "rcn")
                 nc.scalar.activation(out=rcn[:], in_=r1[:], func=ACT.Sqrt, bias=col(eps, E24), scale=1.0)
                 wtile(i, "t1", 2)
-                wtile(i, "t2", 1, tag="t2%d" % (i % 2))
                 b1(i, 0)
-                b2(i, 0)
                 b1(i, 1)
-            if prev:
-                rao = stile(j, "rao")
-                nc.vector.reciprocal(out=rao[:], in_=st[j]["rca"][:])
+            if p2:
+                g_now = USE_G and cur
+                f1(j2, 0)
+                f1(j2, 1)
+                f2(j2, 0, g_now)
+                if not cur:
+                    store_xv_half(j2, 0)
+                f2(j2, 1, g_now)
+                if cur:
+                    store_xv(j2)
+                else:
+                    store_xv_half(j2, 1)
             if cur:
-                b2(i, 1)
-            if prev:
-                nmul(j)
-                e3(j)
-            if cur:
-                b3(i, 0)
                 rno = stile(i, "rno")
                 nc.vector.reciprocal(out=rno[:], in_=st[i]["rcn"][:])
-                b3(i, 1)
-                c2(i)
-                a2(i)
+                wtile(i, "t2", 2)
+                for k in range(4):
+                    b2(i, k)
+            if p1:
+                stile(j1, "ssd")
+                for k in range(4):
+                    e2(j1, k)
+                sdv = stile(j1, "sdv")
+                nc.scalar.activation(
+                    out=sdv[:], in_=st[j1]["ssd"][:], func=ACT.Sqrt, bias=col(eps, E30), scale=1.0 / 255.0
+                )
+                rca = stile(j1, "rca")
+                nc.scalar.activation(out=rca[:], in_=sdv[:], func=ACT.Identity, bias=col(eps, E8), scale=1.0)
+            if cur:
+                wtile(i, "pp", 4)
+                a2(i, 0)
+            if p1:
+                rao = stile(j1, "rao")
+                nc.vector.reciprocal(out=rao[:], in_=st[j1]["rca"][:])
+            if cur:
+                a2(i, 1)
                 if i + 1 < NSUB:
                     pe(i + 1, "pv")
-            if prev:
-                d2(j, 1, "t2%d" % (i % 2), 1)
+            if p1:
+                nma = stile(j1, "nma")
+                nc.vector.tensor_tensor(out=nma[:], in0=st[j1]["negm"][:], in1=st[j1]["rao"][:], op=ALU.mult)
+                for k in range(4):
+                    e3(j1, k)
             if cur:
+                wtile(i, "xk", 3)
+                for k in range(4):
+                    b3(i, k)
+                store_xk(i)
                 d1(i, 0)
                 d1(i, 1)
-            if prev:
-                if cur:
-                    f1(j, 0)
-                    f1(j, 1)
-                    f2(j, 0, G_F2)
-                    f2(j, 1, G_F2)
-                    store_xv(j)
-                else:
-                    f1(j, 0)
-                    f1(j, 1)
-                    f2(j, 0, False)
-                    store_xv_half(j, 0)
-                    f2(j, 1, False)
-                    store_xv_half(j, 1)
-            if cur:
-                d2(i, 0, "xw", 2)
+                tok = work.tile([P, 1], F32, name="tok%d" % i, tag="xa%d" % (i % 3), bufs=1)
+                nc.vector.memset(tok[:], 0.0)
+                d2(i, 0, USE_G)
+                d2(i, 1, USE_G)
                 stile(i, "negm")
-                stile(i, "ssd")
                 for k in range(4):
                     e1(i, k)
-                for k in range(4):
-                    e2(i, k)

@@ -19,6 +19,7 @@ NCH = 8
 NSUB = 16
 WBUF = 3
 USE_G = True
+NWARM = 10
 
 E24 = 0
 NE24 = 1
@@ -171,6 +172,9 @@ def tile_tttwrapper_pa_kernel(
         put_w(0)
         put_w(1)
         put_w(2)
+        warm = psum.tile([P, 512], F32, name="warm", tag="pk", bufs=2)
+        for r in range(NWARM):
+            nc.tensor.matmul(out=warm[:], lhsT=ones[:], rhs=fc[:], start=True, stop=True)
 
         SH4 = [P, 2, 128, 2]
         SH3 = [P, 128, 2]
@@ -347,9 +351,9 @@ def tile_tttwrapper_pa_kernel(
 
         pe(0, "pk")
         pe(0, "pv")
-        for i in range(NSUB + 2):
+        for i in range(NSUB + 1):
             cur = i < NSUB
-            p1 = 1 <= i <= NSUB
+            p1 = 1 <= i < NSUB
             p2 = i >= 2
             j1 = i - 1
             j2 = i - 2
@@ -430,3 +434,38 @@ def tile_tttwrapper_pa_kernel(
                 stile(i, "negm")
                 for k in range(4):
                     e1(i, k)
+
+        L = NSUB - 1
+        uu = work.tile([P, 2, 512], F32, name="uu", tag="t1", bufs=2)
+        ppl = st[L]["pp"]
+        for k in range(4):
+            t, h = divmod(k, 2)
+            nc.vector.scalar_tensor_tensor(
+                out=uu[:, t, hsl(h)],
+                in0=ppl[:, t, hsl(h)],
+                scalar=col(st[L]["negm"], k),
+                in1=twt[L // 2][:, hsl(h)],
+                op0=ALU.add,
+                op1=ALU.mult,
+            )
+        stile(L, "ssd")
+        for k in range(4):
+            e2(L, k)
+        sdl = stile(L, "sdv")
+        nc.scalar.activation(out=sdl[:], in_=st[L]["ssd"][:], func=ACT.Sqrt, bias=col(eps, E30), scale=1.0 / 255.0)
+        rcl = stile(L, "rca")
+        nc.scalar.activation(out=rcl[:], in_=sdl[:], func=ACT.Identity, bias=col(eps, E8), scale=1.0)
+        ral = stile(L, "rao")
+        nc.vector.reciprocal(out=ral[:], in_=rcl[:])
+        for k in range(4):
+            t, h = divmod(k, 2)
+            nc.vector.scalar_tensor_tensor(
+                out=ppl[:, t, hsl(h)],
+                in0=uu[:, t, hsl(h)],
+                scalar=col(ral, k),
+                in1=st[L]["xb%d" % t][:, hsl(h)],
+                op0=ALU.mult,
+                op1=ALU.add,
+            )
+            if h == 1:
+                store_xv_half(L, t)

@@ -19,7 +19,6 @@ NCH = 8
 NSUB = 16
 WBUF = 3
 USE_G = True
-NWARM = 10
 
 E24 = 0
 NE24 = 1
@@ -61,7 +60,10 @@ def tile_tttwrapper_pa_kernel(
         for r in range(2):
             hc_t = const.tile([P, G, 512], U8, name="hc%d" % r, tag="hc%d" % r, align_bytes=64)
             hcb.append(hc_t)
-        hs = const.tile([P, G, 512], U8, name="hs", tag="hs", align_bytes=64)
+        hsb = []
+        for r in range(2):
+            hs_t = const.tile([P, G, 256], U8, name="hs%d" % r, tag="hs%d" % r, align_bytes=64)
+            hsb.append(hs_t)
         ksc = []
         vsc = []
         for r in range(WBUF):
@@ -111,8 +113,9 @@ def tile_tttwrapper_pa_kernel(
 
         nc.gpsimd.memset(wrow[:].bitcast(F32), 0.0)
         make_identity(nc, ident[:])
-        nc.vector.memset(hs[:].bitcast(I32), 0)
+        nc.vector.memset(hsb[0][:].bitcast(I32), 0)
         nc.vector.memset(ksc[0][:].bitcast(I32), 0)
+        nc.vector.memset(hsb[1][:].bitcast(I32), 0)
         nc.vector.memset(ones[:], 1.0)
         nc.vector.memset(eps[:, E24 : E24 + 1], 1e-24)
         nc.vector.memset(eps[:, NE24 : NE24 + 1], -1e-24)
@@ -129,13 +132,14 @@ def tile_tttwrapper_pa_kernel(
         )
         load_codes(hcb[0], hidden_states_words, slice(0, 512))
         load_codes(kc0, wk_w_words, slice(0, 1024))
-        load_scales(hs, hidden_states_scales, slice(0, 512))
+        load_scales(hsb[0], hidden_states_scales, slice(0, 256))
         nc.sync.dma_start(out=wrow[0:1, :], in_=wflat.rearrange("(o n) -> o n", o=1))
         load_scales(ksc[0], wk_w_scales, slice(0, 512))
         load_table(bk, wk_b, 0, 512)
         load_scales(vsc[0], wv_w_scales, slice(0, 512))
         load_codes(vc0, wv_w_words, slice(0, 1024))
         load_table(bv, wv_b, 0, 512)
+        load_scales(hsb[1], hidden_states_scales, slice(256, 512))
         load_codes(hcb[1], hidden_states_words, slice(512, 1024))
         load_table(bt, bflat, 0, 512)
         load_chunk(1)
@@ -172,9 +176,6 @@ def tile_tttwrapper_pa_kernel(
         put_w(0)
         put_w(1)
         put_w(2)
-        warm = psum.tile([P, 512], F32, name="warm", tag="pk", bufs=2)
-        for r in range(NWARM):
-            nc.tensor.matmul(out=warm[:], lhsT=ones[:], rhs=fc[:], start=True, stop=True)
 
         SH4 = [P, 2, 128, 2]
         SH3 = [P, 128, 2]
@@ -193,13 +194,12 @@ def tile_tttwrapper_pa_kernel(
             planes = (ksc if kind == "pk" else vsc)[c % WBUF]
             res = []
             for t in range(2):
-                m = 2 * b + t
                 acc = psum.tile([P, 512], F32, name="%s_%d_%d" % (kind, s, t), tag=kind, bufs=2)
                 for g in range(G):
                     nc.tensor.matmul_mx(
                         out=acc[:],
                         lhsT=hcb[b][:, g, 256 * t : 256 * t + 256].bitcast(FP4),
-                        lhsT_scale=hs[:, g, 128 * m : 128 * m + 128],
+                        lhsT_scale=hsb[b][:, g, 128 * t : 128 * t + 128],
                         rhs=codes[:, g, :].bitcast(FP4),
                         rhs_scale=planes[:, g, :],
                         start=(g == 0),
@@ -374,9 +374,6 @@ def tile_tttwrapper_pa_kernel(
                 nc.scalar.activation(out=r1[:], in_=st[i]["ss"][:], func=ACT.Relu, bias=col(eps, NE24), scale=1.0)
                 rcn = stile(i, "rcn")
                 nc.scalar.activation(out=rcn[:], in_=r1[:], func=ACT.Sqrt, bias=col(eps, E24), scale=1.0)
-                wtile(i, "t1", 2)
-                b1(i, 0)
-                b1(i, 1)
             if p2:
                 g_now = USE_G and cur
                 f1(j2, 0)
@@ -390,6 +387,9 @@ def tile_tttwrapper_pa_kernel(
                 else:
                     store_xv_half(j2, 1)
             if cur:
+                wtile(i, "t1", 2)
+                b1(i, 0)
+                b1(i, 1)
                 rno = stile(i, "rno")
                 nc.vector.reciprocal(out=rno[:], in_=st[i]["rcn"][:])
                 wtile(i, "t2", 2)

@@ -18,7 +18,8 @@ G = 8
 NCH = 8
 NSUB = 16
 WBUF = 3
-USE_G = True
+LEAD = 3
+NXB = LEAD + 2
 
 E24 = 0
 NE24 = 1
@@ -96,19 +97,19 @@ def tile_tttwrapper_pa_kernel(
         def load_table(dst, src, lo, hi):
             nc.sync.dma_start(out=dst[:, lo:hi], in_=src[lo:hi].partition_broadcast(P))
 
-        wcodes = {}
+        kcodes = {}
+        vcodes = {}
 
-        def alloc_codes(c):
+        def load_k(c):
             kc = wpool.tile([P, G, 1024], U8, name="kc%d" % c, tag="kc", align_bytes=64)
-            vc = wpool.tile([P, G, 1024], U8, name="vc%d" % c, tag="vc", align_bytes=64)
-            wcodes[c] = (kc, vc)
-            return kc, vc
-
-        def load_chunk(c):
-            kc, vc = alloc_codes(c)
+            kcodes[c] = kc
             load_scales(ksc[c % WBUF], wk_w_scales, slice(512 * c, 512 * c + 512))
-            load_scales(vsc[c % WBUF], wv_w_scales, slice(512 * c, 512 * c + 512))
             load_codes(kc, wk_w_words, slice(1024 * c, 1024 * c + 1024))
+
+        def load_v(c):
+            vc = wpool.tile([P, G, 1024], U8, name="vc%d" % c, tag="vc", align_bytes=64)
+            vcodes[c] = vc
+            load_scales(vsc[c % WBUF], wv_w_scales, slice(512 * c, 512 * c + 512))
             load_codes(vc, wv_w_words, slice(1024 * c, 1024 * c + 1024))
 
         nc.gpsimd.memset(wrow[:].bitcast(F32), 0.0)
@@ -121,12 +122,12 @@ def tile_tttwrapper_pa_kernel(
         nc.vector.memset(eps[:, NE24 : NE24 + 1], -1e-24)
         nc.vector.memset(eps[:, E30 : E30 + 1], 1e-30)
         nc.vector.memset(eps[:, E8 : E8 + 1], 1e-8)
-        nc.vector.memset(vsc[0][:].bitcast(I32), 0)
         nc.vector.memset(ksc[1][:].bitcast(I32), 0)
-        nc.vector.memset(vsc[1][:].bitcast(I32), 0)
+        nc.vector.memset(vsc[0][:].bitcast(I32), 0)
         nc.scalar.activation(out=scr[:], in_=eps[:, E8 : E8 + 1], func=ACT.Sqrt)
 
-        kc0, vc0 = alloc_codes(0)
+        kc0 = wpool.tile([P, G, 1024], U8, name="kc0", tag="kc", align_bytes=64)
+        kcodes[0] = kc0
         nc.sync.dma_start(
             out=fc[:].rearrange("p (t n) -> p t n", t=2), in_=freqs_cis.rearrange("(t p) j e -> p t (j e)", p=P)
         )
@@ -136,24 +137,27 @@ def tile_tttwrapper_pa_kernel(
         nc.sync.dma_start(out=wrow[0:1, :], in_=wflat.rearrange("(o n) -> o n", o=1))
         load_scales(ksc[0], wk_w_scales, slice(0, 512))
         load_table(bk, wk_b, 0, 512)
-        load_scales(vsc[0], wv_w_scales, slice(0, 512))
-        load_codes(vc0, wv_w_words, slice(0, 1024))
-        load_table(bv, wv_b, 0, 512)
         load_scales(hsb[1], hidden_states_scales, slice(256, 512))
         load_codes(hcb[1], hidden_states_words, slice(512, 1024))
+        load_table(bk, wk_b, 512, 1024)
+        load_k(1)
+        load_table(bv, wv_b, 0, 512)
         load_table(bt, bflat, 0, 512)
-        load_chunk(1)
-        load_table(bk, wk_b, 512, 4096)
+        load_v(0)
         load_table(bv, wv_b, 512, 4096)
         load_table(bt, bflat, 512, 4096)
+        load_table(bk, wk_b, 1024, 4096)
 
         fcv = fc[:].rearrange("p (n e) -> p n e", e=2)
         fc2v = fc2[:].rearrange("p (n e) -> p n e", e=2)
         nc.vector.tensor_scalar_mul(out=fc2v[:, :, 0:1], in0=fcv[:, :, 1:2], scalar1=-1.0)
         nc.vector.tensor_copy(out=fc2v[:, :, 1:2], in_=fcv[:, :, 0:1])
         nc.vector.memset(ksc[2][:].bitcast(I32), 0)
+        nc.vector.memset(vsc[1][:].bitcast(I32), 0)
         nc.vector.memset(vsc[2][:].bitcast(I32), 0)
-        load_chunk(2)
+        load_k(2)
+        load_v(1)
+        load_v(2)
 
         nc.tensor.matmul(out=tbl[:, 0:512], lhsT=ident[:], rhs=fc[:], start=True, stop=True)
         nc.tensor.matmul(out=tbl[:, 512:1024], lhsT=ident[:], rhs=fc2[:], start=True, stop=True)
@@ -187,14 +191,21 @@ def tile_tttwrapper_pa_kernel(
             return ap.rearrange("p (j e) -> p j e", e=2)
 
         st = {}
+        for s in range(NSUB):
+            st[s] = {}
 
-        def pe(s, kind):
+        def ok(s):
+            return 0 <= s < NSUB
+
+        def pe(s, kind, tag=None):
+            if not ok(s):
+                return
             c, b = divmod(s, 2)
-            codes = wcodes[c][0 if kind == "pk" else 1]
+            codes = (kcodes if kind == "pk" else vcodes)[c]
             planes = (ksc if kind == "pk" else vsc)[c % WBUF]
             res = []
             for t in range(2):
-                acc = psum.tile([P, 512], F32, name="%s_%d_%d" % (kind, s, t), tag=kind, bufs=2)
+                acc = psum.tile([P, 512], F32, name="%s_%d_%d" % (kind, s, t), tag=(tag or kind), bufs=2)
                 for g in range(G):
                     nc.tensor.matmul_mx(
                         out=acc[:],
@@ -206,8 +217,6 @@ def tile_tttwrapper_pa_kernel(
                         stop=(g == G - 1),
                     )
                 res.append(acc)
-            if s not in st:
-                st[s] = {}
             st[s][kind] = res
 
         def cols(s):
@@ -223,14 +232,16 @@ def tile_tttwrapper_pa_kernel(
             return slice(256 * b, 256 * b + 256)
 
         def wtile(s, nm, bufs):
-            tl = work.tile([P, 2, 512], F32, name="%s%d" % (nm, s), tag=nm, bufs=bufs)
-            st[s][nm] = tl
-            return tl
+            if nm not in st[s]:
+                tl = work.tile([P, 2, 512], F32, name="%s%d" % (nm, s), tag=nm, bufs=bufs)
+                st[s][nm] = tl
+            return st[s][nm]
 
         def stile(s, nm):
-            tl = small.tile([P, 4], F32, name="%s%d" % (nm, s), tag=nm, bufs=4)
-            st[s][nm] = tl
-            return tl
+            if nm not in st[s]:
+                tl = small.tile([P, 4], F32, name="%s%d" % (nm, s), tag=nm, bufs=4)
+                st[s][nm] = tl
+            return st[s][nm]
 
         def junk():
             return work.tile([P, 256], F32, name="junk", tag="junk", bufs=4)
@@ -242,230 +253,461 @@ def tile_tttwrapper_pa_kernel(
             return tl[:, k : k + 1]
 
         def a1(s, t):
-            nc.vector.tensor_tensor(out=st[s]["k0"][:, t, :], in0=st[s]["pk"][t][:], in1=bk[:, cols(s)], op=ALU.add)
+            if not ok(s):
+                return
+            k0 = wtile(s, "k0", 2)
+            nc.vector.tensor_tensor(out=k0[:, t, :], in0=st[s]["pk"][t][:], in1=bk[:, cols(s)], op=ALU.add)
 
-        def a2(s, t):
-            nc.vector.tensor_tensor(out=st[s]["pp"][:, t, :], in0=st[s]["pv"][t][:], in1=bv[:, cols(s)], op=ALU.add)
+        def c1(s, t):
+            if not ok(s):
+                return
+            ss = stile(s, "ss")
+            for h in range(2):
+                jk = junk()
+                nc.scalar.activation(
+                    out=jk[:], in_=st[s]["k0"][:, t, hsl(h)], func=ACT.Square, accum_out=col(ss, 2 * t + h)
+                )
 
-        def c1(s, k):
-            t, h = divmod(k, 2)
-            jk = junk()
-            nc.scalar.activation(
-                out=jk[:], in_=st[s]["k0"][:, t, hsl(h)], func=ACT.Square, accum_out=col(st[s]["ss"], k)
-            )
+        def c2(s):
+            if not ok(s):
+                return
+            r1 = stile(s, "r1")
+            nc.scalar.activation(out=r1[:], in_=st[s]["ss"][:], func=ACT.Relu, bias=col(eps, NE24), scale=1.0)
+            rcn = stile(s, "rcn")
+            nc.scalar.activation(out=rcn[:], in_=r1[:], func=ACT.Sqrt, bias=col(eps, E24), scale=1.0)
+
+        def c3(s):
+            if not ok(s):
+                return
+            rno = stile(s, "rno")
+            nc.vector.reciprocal(out=rno[:], in_=st[s]["rcn"][:])
 
         def b1(s, t):
+            if not ok(s):
+                return
+            t1 = wtile(s, "t1", 2)
             nc.vector.tensor_tensor(
-                out=v4(st[s]["t1"][:, t, :]),
+                out=v4(t1[:, t, :]),
                 in0=v4(st[s]["k0"][:, t, :])[:, :, :, 0:1].to_broadcast(SH4),
                 in1=v3(tbl[:, 256 * t : 256 * t + 256]).unsqueeze(1).to_broadcast(SH4),
                 op=ALU.mult,
             )
 
-        def b2(s, k):
-            t, h = divmod(k, 2)
-            nc.vector.scalar_tensor_tensor(
-                out=v3(st[s]["t2"][:, t, hsl(h)]),
-                in0=v3(st[s]["k0"][:, t, hsl(h)])[:, :, 1:2].to_broadcast(SH3),
-                scalar=col(st[s]["rno"], k),
-                in1=v3(tbl[:, 512 + 256 * t : 512 + 256 * t + 256]),
-                op0=ALU.mult,
-                op1=ALU.mult,
-            )
+        def b2(s, t):
+            if not ok(s):
+                return
+            t2 = wtile(s, "t2", 2)
+            for h in range(2):
+                nc.vector.scalar_tensor_tensor(
+                    out=v3(t2[:, t, hsl(h)]),
+                    in0=v3(st[s]["k0"][:, t, hsl(h)])[:, :, 1:2].to_broadcast(SH3),
+                    scalar=col(st[s]["rno"], 2 * t + h),
+                    in1=v3(tbl[:, 512 + 256 * t : 512 + 256 * t + 256]),
+                    op0=ALU.mult,
+                    op1=ALU.mult,
+                )
 
-        def b3(s, k):
-            t, h = divmod(k, 2)
-            nc.vector.scalar_tensor_tensor(
-                out=st[s]["xk"][:, t, hsl(h)],
-                in0=st[s]["t1"][:, t, hsl(h)],
-                scalar=col(st[s]["rno"], k),
-                in1=st[s]["t2"][:, t, hsl(h)],
-                op0=ALU.mult,
-                op1=ALU.add,
-            )
+        def b3(s, t):
+            if not ok(s):
+                return
+            xk = wtile(s, "xk", 3)
+            for h in range(2):
+                nc.vector.scalar_tensor_tensor(
+                    out=xk[:, t, hsl(h)],
+                    in0=st[s]["t1"][:, t, hsl(h)],
+                    scalar=col(st[s]["rno"], 2 * t + h),
+                    in1=st[s]["t2"][:, t, hsl(h)],
+                    op0=ALU.mult,
+                    op1=ALU.add,
+                )
 
         def store_xk(s):
+            if not ok(s):
+                return
             nc.sync.dma_start(out=o0[rows2(s), cols(s)].rearrange("(t p) n -> p t n", p=P), in_=st[s]["xk"][:])
 
-        def d1(s, t):
-            pp = st[s]["pp"]
-            nc.vector.tensor_tensor(out=pp[:, t, :], in0=pp[:, t, :], in1=st[s]["xk"][:, t, :], op=ALU.subtract)
+        def mk(s, t, eng):
+            if not ok(s):
+                return
+            mm = wtile(s, "mm", LEAD + 1)
+            eng.tensor_tensor(out=mm[:, t, :], in0=st[s]["xk"][:, t, :], in1=bv[:, cols(s)], op=ALU.subtract)
 
-        def d2(s, t, on_g):
+        def token(s):
+            if not ok(s):
+                return
+            tok = work.tile([P, 1], F32, name="tok%d" % s, tag="xa%d" % (s % NXB), bufs=1)
+            nc.vector.memset(tok[:], 0.0)
+
+        def d2(s, t, eng):
+            if not ok(s):
+                return
             if t == 0:
-                xb = work.tile([P, 512], F32, name="xb0_%d" % s, tag="xa%d" % (s % 3), bufs=1)
+                xb = work.tile([P, 512], F32, name="xb0_%d" % s, tag="xa%d" % (s % NXB), bufs=1)
             else:
-                xb = work.tile([P, 512], F32, name="xb1_%d" % s, tag="xc", bufs=3)
+                xb = work.tile([P, 512], F32, name="xb1_%d" % s, tag="xc", bufs=NXB)
             st[s]["xb%d" % t] = xb
-            eng = nc.gpsimd if on_g else nc.vector
             eng.tensor_tensor(out=xb[:], in0=st[s]["xk"][:, t, :], in1=bt[:, cols(s)], op=ALU.add)
 
-        def e1(s, k):
-            t, h = divmod(k, 2)
-            jk = junk()
-            nc.scalar.activation(
-                out=jk[:],
-                in_=st[s]["pp"][:, t, hsl(h)],
-                func=ACT.Identity,
-                scale=-1.0 / 256.0,
-                accum_out=col(st[s]["negm"], k),
+        def df(s, t):
+            if not ok(s):
+                return
+            pp = wtile(s, "pp", 4)
+            nc.vector.tensor_tensor(out=pp[:, t, :], in0=st[s]["pv"][t][:], in1=st[s]["mm"][:, t, :], op=ALU.subtract)
+
+        def dfa(s, t):
+            pp = wtile(s, "pp", 4)
+            sm = stile(s, "sm")
+            for h in range(2):
+                nc.vector.scalar_tensor_tensor(
+                    out=pp[:, t, hsl(h)],
+                    in0=st[s]["pv"][t][:, hsl(h)],
+                    scalar=1.0,
+                    in1=st[s]["mm"][:, t, hsl(h)],
+                    op0=ALU.mult,
+                    op1=ALU.subtract,
+                    accum_out=col(sm, 2 * t + h),
+                )
+
+        def ngm(s, t):
+            negm = stile(s, "negm")
+            nc.vector.tensor_scalar_mul(
+                out=negm[:, 2 * t : 2 * t + 2], in0=st[s]["sm"][:, 2 * t : 2 * t + 2], scalar1=-1.0 / 256.0
             )
 
-        def e2(s, k):
-            t, h = divmod(k, 2)
-            jk = junk()
+        def sq(s, t):
+            sdv = stile(s, "sdv")
             nc.scalar.activation(
-                out=jk[:],
-                in_=st[s]["pp"][:, t, hsl(h)],
-                func=ACT.Square,
-                bias=col(st[s]["negm"], k),
-                scale=1.0,
-                accum_out=col(st[s]["ssd"], k),
+                out=sdv[:, 2 * t : 2 * t + 2], in_=st[s]["ssd"][:, 2 * t : 2 * t + 2], func=ACT.Sqrt, bias=col(eps, E30), scale=1.0 / 255.0
             )
 
-        def e3(s, k):
-            t, h = divmod(k, 2)
+        def radd(s, t):
+            rca = stile(s, "rca")
+            nc.vector.tensor_scalar_add(out=rca[:, 2 * t : 2 * t + 2], in0=st[s]["sdv"][:, 2 * t : 2 * t + 2], scalar1=1e-8)
+
+        def rinv(s, t):
+            rao = stile(s, "rao")
+            nc.vector.reciprocal(out=rao[:, 2 * t : 2 * t + 2], in_=st[s]["rca"][:, 2 * t : 2 * t + 2])
+
+        def sdt(s, t):
+            sdv = stile(s, "sdv")
+            nc.scalar.activation(
+                out=sdv[:, 2 * t : 2 * t + 2], in_=st[s]["ssd"][:, 2 * t : 2 * t + 2], func=ACT.Sqrt, bias=col(eps, E30), scale=1.0 / 255.0
+            )
+            rca = stile(s, "rca")
+            nc.scalar.activation(out=rca[:, 2 * t : 2 * t + 2], in_=sdv[:, 2 * t : 2 * t + 2], func=ACT.Identity, bias=col(eps, E8), scale=1.0)
+
+        def rat(s, t):
+            rca = stile(s, "rca")
+            rao = stile(s, "rao")
+            nc.vector.reciprocal(out=rao[:, 2 * t : 2 * t + 2], in_=rca[:, 2 * t : 2 * t + 2])
+
+        def e1(s, t):
+            if not ok(s):
+                return
+            negm = stile(s, "negm")
+            for h in range(2):
+                jk = junk()
+                nc.scalar.activation(
+                    out=jk[:],
+                    in_=st[s]["pp"][:, t, hsl(h)],
+                    func=ACT.Identity,
+                    scale=-1.0 / 256.0,
+                    accum_out=col(negm, 2 * t + h),
+                )
+
+        def e2a(s, t):
+            if not ok(s):
+                return
             pp = st[s]["pp"]
+            for h in range(2):
+                nc.scalar.activation(
+                    out=pp[:, t, hsl(h)],
+                    in_=pp[:, t, hsl(h)],
+                    func=ACT.Identity,
+                    bias=col(st[s]["negm"], 2 * t + h),
+                    scale=1.0,
+                )
+
+        def e2b(s, t):
+            if not ok(s):
+                return
+            ssd = stile(s, "ssd")
+            for h in range(2):
+                jk = junk()
+                nc.scalar.activation(
+                    out=jk[:], in_=st[s]["pp"][:, t, hsl(h)], func=ACT.Square, accum_out=col(ssd, 2 * t + h)
+                )
+
+        def e2(s, t):
+            ssd = stile(s, "ssd")
+            for h in range(2):
+                jk = junk()
+                nc.scalar.activation(
+                    out=jk[:],
+                    in_=st[s]["pp"][:, t, hsl(h)],
+                    func=ACT.Square,
+                    bias=col(st[s]["negm"], 2 * t + h),
+                    scale=1.0,
+                    accum_out=col(ssd, 2 * t + h),
+                )
+
+        def sd(s, lo, hi):
+            if not ok(s):
+                return
+            sdv = stile(s, "sdv")
             nc.scalar.activation(
-                out=pp[:, t, hsl(h)],
-                in_=pp[:, t, hsl(h)],
-                func=ACT.Identity,
-                bias=col(st[s]["nma"], k),
-                scale=col(st[s]["rao"], k),
+                out=sdv[:, lo:hi], in_=st[s]["ssd"][:, lo:hi], func=ACT.Sqrt, bias=col(eps, E30), scale=1.0 / 255.0
             )
+            rca = stile(s, "rca")
+            nc.scalar.activation(out=rca[:, lo:hi], in_=sdv[:, lo:hi], func=ACT.Identity, bias=col(eps, E8), scale=1.0)
+
+        def ra(s, lo, hi):
+            if not ok(s):
+                return
+            rao = stile(s, "rao")
+            nc.vector.reciprocal(out=rao[:, lo:hi], in_=st[s]["rca"][:, lo:hi])
 
         def f1(s, t):
+            if not ok(s):
+                return
             pp = st[s]["pp"]
-            nc.vector.tensor_tensor(out=pp[:, t, :], in0=pp[:, t, :], in1=twt[s // 2], op=ALU.mult)
+            for h in range(2):
+                nc.vector.scalar_tensor_tensor(
+                    out=pp[:, t, hsl(h)],
+                    in0=pp[:, t, hsl(h)],
+                    scalar=col(st[s]["rao"], 2 * t + h),
+                    in1=twt[s // 2][:, hsl(h)],
+                    op0=ALU.mult,
+                    op1=ALU.mult,
+                )
 
-        def f2(s, t, on_g):
+        def f2(s, t, eng):
+            if not ok(s):
+                return
             pp = st[s]["pp"]
-            eng = nc.gpsimd if on_g else nc.vector
             eng.tensor_tensor(out=pp[:, t, :], in0=pp[:, t, :], in1=st[s]["xb%d" % t][:], op=ALU.add)
 
         def store_xv(s):
+            if not ok(s):
+                return
             nc.sync.dma_start(out=o1[rows2(s), cols(s)].rearrange("(t p) n -> p t n", p=P), in_=st[s]["pp"][:])
 
         def store_xv_half(s, t):
             nc.sync.dma_start(out=o1[rows(s, t), cols(s)], in_=st[s]["pp"][:, t, :])
 
-        pe(0, "pk")
-        pe(0, "pv")
-        for i in range(NSUB + 1):
-            cur = i < NSUB
-            p1 = 1 <= i < NSUB
-            p2 = i >= 2
-            j1 = i - 1
-            j2 = i - 2
-            if i % 2 == 1 and (i // 2) + 3 < NCH:
-                load_chunk((i // 2) + 3)
-            if cur:
-                wtile(i, "k0", 2)
-                a1(i, 0)
-                a1(i, 1)
-                if i == 6:
-                    put_w(3)
-                if i + 1 < NSUB:
-                    pe(i + 1, "pk")
-                stile(i, "ss")
-                for k in range(4):
-                    c1(i, k)
-                r1 = stile(i, "r1")
-                nc.scalar.activation(out=r1[:], in_=st[i]["ss"][:], func=ACT.Relu, bias=col(eps, NE24), scale=1.0)
-                rcn = stile(i, "rcn")
-                nc.scalar.activation(out=rcn[:], in_=r1[:], func=ACT.Sqrt, bias=col(eps, E24), scale=1.0)
-            if p2:
-                g_now = USE_G and cur
-                f1(j2, 0)
-                f1(j2, 1)
-                f2(j2, 0, g_now)
-                if not cur:
-                    store_xv_half(j2, 0)
-                f2(j2, 1, g_now)
-                if cur:
-                    store_xv(j2)
-                else:
-                    store_xv_half(j2, 1)
-            if cur:
-                wtile(i, "t1", 2)
-                b1(i, 0)
-                b1(i, 1)
-                rno = stile(i, "rno")
-                nc.vector.reciprocal(out=rno[:], in_=st[i]["rcn"][:])
-                wtile(i, "t2", 2)
-                for k in range(4):
-                    b2(i, k)
-            if p1:
-                stile(j1, "ssd")
-                for k in range(4):
-                    e2(j1, k)
-                sdv = stile(j1, "sdv")
-                nc.scalar.activation(
-                    out=sdv[:], in_=st[j1]["ssd"][:], func=ACT.Sqrt, bias=col(eps, E30), scale=1.0 / 255.0
+        def uu(s, t):
+            u = wtile(s, "t1u", 1)
+            for h in range(2):
+                nc.vector.scalar_tensor_tensor(
+                    out=u[:, t, hsl(h)],
+                    in0=st[s]["pp"][:, t, hsl(h)],
+                    scalar=col(st[s]["negm"], 2 * t + h),
+                    in1=twt[s // 2][:, hsl(h)],
+                    op0=ALU.add,
+                    op1=ALU.mult,
                 )
-                rca = stile(j1, "rca")
-                nc.scalar.activation(out=rca[:], in_=sdv[:], func=ACT.Identity, bias=col(eps, E8), scale=1.0)
-            if cur:
-                wtile(i, "pp", 4)
-                a2(i, 0)
-            if p1:
-                rao = stile(j1, "rao")
-                nc.vector.reciprocal(out=rao[:], in_=st[j1]["rca"][:])
-            if cur:
-                a2(i, 1)
-                if i + 1 < NSUB:
-                    pe(i + 1, "pv")
-            if p1:
-                nma = stile(j1, "nma")
-                nc.vector.tensor_tensor(out=nma[:], in0=st[j1]["negm"][:], in1=st[j1]["rao"][:], op=ALU.mult)
-                for k in range(4):
-                    e3(j1, k)
-            if cur:
-                wtile(i, "xk", 3)
-                for k in range(4):
-                    b3(i, k)
-                store_xk(i)
-                d1(i, 0)
-                d1(i, 1)
-                tok = work.tile([P, 1], F32, name="tok%d" % i, tag="xa%d" % (i % 3), bufs=1)
-                nc.vector.memset(tok[:], 0.0)
-                d2(i, 0, USE_G)
-                d2(i, 1, USE_G)
-                stile(i, "negm")
-                for k in range(4):
-                    e1(i, k)
 
-        L = NSUB - 1
-        uu = work.tile([P, 2, 512], F32, name="uu", tag="t1", bufs=2)
-        ppl = st[L]["pp"]
-        for k in range(4):
-            t, h = divmod(k, 2)
-            nc.vector.scalar_tensor_tensor(
-                out=uu[:, t, hsl(h)],
-                in0=ppl[:, t, hsl(h)],
-                scalar=col(st[L]["negm"], k),
-                in1=twt[L // 2][:, hsl(h)],
-                op0=ALU.add,
-                op1=ALU.mult,
-            )
-        stile(L, "ssd")
-        for k in range(4):
-            e2(L, k)
-        sdl = stile(L, "sdv")
-        nc.scalar.activation(out=sdl[:], in_=st[L]["ssd"][:], func=ACT.Sqrt, bias=col(eps, E30), scale=1.0 / 255.0)
-        rcl = stile(L, "rca")
-        nc.scalar.activation(out=rcl[:], in_=sdl[:], func=ACT.Identity, bias=col(eps, E8), scale=1.0)
-        ral = stile(L, "rao")
-        nc.vector.reciprocal(out=ral[:], in_=rcl[:])
-        for k in range(4):
-            t, h = divmod(k, 2)
-            nc.vector.scalar_tensor_tensor(
-                out=ppl[:, t, hsl(h)],
-                in0=uu[:, t, hsl(h)],
-                scalar=col(ral, k),
-                in1=st[L]["xb%d" % t][:, hsl(h)],
-                op0=ALU.mult,
-                op1=ALU.add,
-            )
-            if h == 1:
-                store_xv_half(L, t)
+        def fin(s, t):
+            for h in range(2):
+                nc.vector.scalar_tensor_tensor(
+                    out=st[s]["pp"][:, t, hsl(h)],
+                    in0=st[s]["t1u"][:, t, hsl(h)],
+                    scalar=col(st[s]["rao"], 2 * t + h),
+                    in1=st[s]["xb%d" % t][:, hsl(h)],
+                    op0=ALU.mult,
+                    op1=ALU.add,
+                )
+
+        GP = nc.gpsimd
+        VE = nc.vector
+
+        pe(0, "pk")
+        a1(0, 0)
+        c1(0, 0)
+        b1(0, 0)
+        a1(0, 1)
+        c1(0, 1)
+        c2(0)
+        b1(0, 1)
+        pe(1, "pk")
+        a1(1, 0)
+        c1(1, 0)
+        c3(0)
+        b2(0, 0)
+        b2(0, 1)
+        a1(1, 1)
+        c1(1, 1)
+        c2(1)
+        b3(0, 0)
+        b3(0, 1)
+        store_xk(0)
+        load_k(3)
+        pe(2, "pk")
+        a1(2, 0)
+        c1(2, 0)
+        mk(0, 0, VE)
+        mk(0, 1, VE)
+        token(0)
+        d2(0, 0, GP)
+        d2(0, 1, GP)
+        b1(1, 0)
+        a1(2, 1)
+        c1(2, 1)
+        c2(2)
+        b1(1, 1)
+        c3(1)
+        b2(1, 0)
+        b2(1, 1)
+        b3(1, 0)
+        b3(1, 1)
+        store_xk(1)
+        mk(1, 0, VE)
+        mk(1, 1, VE)
+        token(1)
+        d2(1, 0, GP)
+        d2(1, 1, GP)
+        b1(2, 0)
+        b1(2, 1)
+
+        for i in range(0, NSUB - LEAD):
+            a = i + LEAD
+            n = a - 1
+            j = i - 1
+            if a % 2 == 0 and a // 2 + 2 < NCH:
+                load_k(a // 2 + 2)
+            if i % 2 == 0 and i >= 2 and i // 2 + 2 < NCH:
+                load_v(i // 2 + 2)
+            if i == 6:
+                put_w(3)
+            pe(a, "pk")
+            df(j, 1)
+            pe(i, "pv")
+            e1(j, 1)
+            e2a(j, 1)
+            e2b(j, 1)
+            sd(j, 0, 4)
+            late = i == 0
+            if late:
+                a1(a, 0)
+                c1(a, 0)
+            c3(n)
+            b2(n, 0)
+            b2(n, 1)
+            if late:
+                a1(a, 1)
+                c1(a, 1)
+                c2(a)
+            b3(n, 0)
+            if not late:
+                a1(a, 0)
+                c1(a, 0)
+            b3(n, 1)
+            store_xk(n)
+            mk(n, 0, VE)
+            mk(n, 1, VE)
+            token(n)
+            d2(n, 0, GP)
+            d2(n, 1, GP)
+            if not late:
+                a1(a, 1)
+                c1(a, 1)
+                c2(a)
+            ra(j, 0, 4)
+            f1(j, 0)
+            f1(j, 1)
+            f2(j, 0, GP)
+            f2(j, 1, GP)
+            store_xv(j)
+            b1(a, 0)
+            df(i, 0)
+            e1(i, 0)
+            e2a(i, 0)
+            e2b(i, 0)
+            b1(a, 1)
+
+        sq(12, 0)
+        dfa(12, 1)
+        pe(13, "pv", "pk")
+        c3(15)
+        ngm(12, 1)
+        e2a(12, 1)
+        e2b(12, 1)
+        sq(12, 1)
+        b2(15, 0)
+        b2(15, 1)
+        b3(15, 0)
+        b3(15, 1)
+        store_xk(15)
+        mk(15, 0, VE)
+        mk(15, 1, VE)
+        token(15)
+        d2(15, 0, GP)
+        d2(15, 1, GP)
+        radd(12, 0)
+        dfa(13, 0)
+        pe(14, "pv")
+        rinv(12, 0)
+        ngm(13, 0)
+        e2a(13, 0)
+        e2b(13, 0)
+        sq(13, 0)
+        radd(12, 1)
+        f1(12, 0)
+        f2(12, 0, GP)
+        rinv(12, 1)
+        dfa(13, 1)
+        pe(15, "pv", "pk")
+        f1(12, 1)
+        f2(12, 1, GP)
+        store_xv(12)
+        ngm(13, 1)
+        e2a(13, 1)
+        e2b(13, 1)
+        sq(13, 1)
+        radd(13, 0)
+        dfa(14, 0)
+        rinv(13, 0)
+        ngm(14, 0)
+        e2a(14, 0)
+        e2b(14, 0)
+        sq(14, 0)
+        f1(13, 0)
+        f2(13, 0, GP)
+        radd(13, 1)
+        dfa(14, 1)
+        rinv(13, 1)
+        ngm(14, 1)
+        e2a(14, 1)
+        e2b(14, 1)
+        sq(14, 1)
+        f1(13, 1)
+        f2(13, 1, GP)
+        store_xv(13)
+        radd(14, 0)
+        dfa(15, 0)
+        rinv(14, 0)
+        ngm(15, 0)
+        e2(15, 0)
+        sq(15, 0)
+        f1(14, 0)
+        f2(14, 0, GP)
+        store_xv_half(14, 0)
+        radd(14, 1)
+        rinv(14, 1)
+        f1(14, 1)
+        f2(14, 1, GP)
+        store_xv_half(14, 1)
+        dfa(15, 1)
+        radd(15, 0)
+        ngm(15, 1)
+        uu(15, 0)
+        e2(15, 1)
+        sq(15, 1)
+        rinv(15, 0)
+        uu(15, 1)
+        fin(15, 0)
+        store_xv_half(15, 0)
+        radd(15, 1)
+        rinv(15, 1)
+        fin(15, 1)
+        store_xv_half(15, 1)

@@ -115,15 +115,12 @@ def tile_tttwrapper_pa_kernel(
         nc.gpsimd.memset(wrow[:].bitcast(F32), 0.0)
         make_identity(nc, ident[:])
         nc.vector.memset(hsb[0][:].bitcast(I32), 0)
-        nc.vector.memset(ksc[0][:].bitcast(I32), 0)
-        nc.vector.memset(hsb[1][:].bitcast(I32), 0)
         nc.vector.memset(ones[:], 1.0)
+        nc.vector.memset(ksc[0][:].bitcast(I32), 0)
         nc.vector.memset(eps[:, E24 : E24 + 1], 1e-24)
         nc.vector.memset(eps[:, NE24 : NE24 + 1], -1e-24)
         nc.vector.memset(eps[:, E30 : E30 + 1], 1e-30)
         nc.vector.memset(eps[:, E8 : E8 + 1], 1e-8)
-        nc.vector.memset(ksc[1][:].bitcast(I32), 0)
-        nc.vector.memset(vsc[0][:].bitcast(I32), 0)
         nc.scalar.activation(out=scr[:], in_=eps[:, E8 : E8 + 1], func=ACT.Sqrt)
 
         kc0 = wpool.tile([P, G, 1024], U8, name="kc0", tag="kc", align_bytes=64)
@@ -132,32 +129,30 @@ def tile_tttwrapper_pa_kernel(
             out=fc[:].rearrange("p (t n) -> p t n", t=2), in_=freqs_cis.rearrange("(t p) j e -> p t (j e)", p=P)
         )
         load_codes(hcb[0], hidden_states_words, slice(0, 512))
-        load_codes(kc0, wk_w_words, slice(0, 1024))
         load_scales(hsb[0], hidden_states_scales, slice(0, 256))
         nc.sync.dma_start(out=wrow[0:1, :], in_=wflat.rearrange("(o n) -> o n", o=1))
+        load_codes(kc0, wk_w_words, slice(0, 1024))
         load_scales(ksc[0], wk_w_scales, slice(0, 512))
         load_table(bk, wk_b, 0, 512)
-        load_scales(hsb[1], hidden_states_scales, slice(256, 512))
-        load_codes(hcb[1], hidden_states_words, slice(512, 1024))
-        load_table(bk, wk_b, 512, 1024)
-        load_k(1)
-        load_table(bv, wv_b, 0, 512)
-        load_table(bt, bflat, 0, 512)
-        load_v(0)
-        load_table(bv, wv_b, 512, 4096)
-        load_table(bt, bflat, 512, 4096)
-        load_table(bk, wk_b, 1024, 4096)
 
         fcv = fc[:].rearrange("p (n e) -> p n e", e=2)
         fc2v = fc2[:].rearrange("p (n e) -> p n e", e=2)
         nc.vector.tensor_scalar_mul(out=fc2v[:, :, 0:1], in0=fcv[:, :, 1:2], scalar1=-1.0)
         nc.vector.tensor_copy(out=fc2v[:, :, 1:2], in_=fcv[:, :, 0:1])
+
+        nc.vector.memset(hsb[1][:].bitcast(I32), 0)
+        load_scales(hsb[1], hidden_states_scales, slice(256, 512))
+        load_codes(hcb[1], hidden_states_words, slice(512, 1024))
+        nc.vector.memset(ksc[1][:].bitcast(I32), 0)
+        load_k(1)
+        load_table(bk, wk_b, 512, 1024)
+        load_table(bv, wv_b, 0, 512)
+        load_table(bt, bflat, 0, 512)
+        nc.vector.memset(vsc[0][:].bitcast(I32), 0)
+        load_v(0)
         nc.vector.memset(ksc[2][:].bitcast(I32), 0)
         nc.vector.memset(vsc[1][:].bitcast(I32), 0)
         nc.vector.memset(vsc[2][:].bitcast(I32), 0)
-        load_k(2)
-        load_v(1)
-        load_v(2)
 
         nc.tensor.matmul(out=tbl[:, 0:512], lhsT=ident[:], rhs=fc[:], start=True, stop=True)
         nc.tensor.matmul(out=tbl[:, 512:1024], lhsT=ident[:], rhs=fc2[:], start=True, stop=True)
@@ -367,26 +362,8 @@ def tile_tttwrapper_pa_kernel(
                     op1=ALU.subtract,
                     accum_out=col(sm, 2 * t + h),
                 )
-
-        def ngm(s, t):
             negm = stile(s, "negm")
-            nc.vector.tensor_scalar_mul(
-                out=negm[:, 2 * t : 2 * t + 2], in0=st[s]["sm"][:, 2 * t : 2 * t + 2], scalar1=-1.0 / 256.0
-            )
-
-        def sq(s, t):
-            sdv = stile(s, "sdv")
-            nc.scalar.activation(
-                out=sdv[:, 2 * t : 2 * t + 2], in_=st[s]["ssd"][:, 2 * t : 2 * t + 2], func=ACT.Sqrt, bias=col(eps, E30), scale=1.0 / 255.0
-            )
-
-        def radd(s, t):
-            rca = stile(s, "rca")
-            nc.vector.tensor_scalar_add(out=rca[:, 2 * t : 2 * t + 2], in0=st[s]["sdv"][:, 2 * t : 2 * t + 2], scalar1=1e-8)
-
-        def rinv(s, t):
-            rao = stile(s, "rao")
-            nc.vector.reciprocal(out=rao[:, 2 * t : 2 * t + 2], in_=st[s]["rca"][:, 2 * t : 2 * t + 2])
+            nc.scalar.activation(out=negm[:, 2 * t : 2 * t + 2], in_=sm[:, 2 * t : 2 * t + 2], func=ACT.Identity, scale=-1.0 / 256.0)
 
         def sdt(s, t):
             sdv = stile(s, "sdv")
@@ -541,7 +518,10 @@ def tile_tttwrapper_pa_kernel(
         b3(0, 0)
         b3(0, 1)
         store_xk(0)
-        load_k(3)
+        load_k(2)
+        load_table(bv, wv_b, 512, 1024)
+        load_table(bt, bflat, 512, 1024)
+        load_table(bk, wk_b, 1024, 1536)
         pe(2, "pk")
         a1(2, 0)
         c1(2, 0)
@@ -561,6 +541,8 @@ def tile_tttwrapper_pa_kernel(
         b3(1, 0)
         b3(1, 1)
         store_xk(1)
+        load_v(1)
+        load_k(3)
         mk(1, 0, VE)
         mk(1, 1, VE)
         token(1)
@@ -597,12 +579,18 @@ def tile_tttwrapper_pa_kernel(
                 a1(a, 1)
                 c1(a, 1)
                 c2(a)
-            b3(n, 0)
             if not late:
                 a1(a, 0)
                 c1(a, 0)
+            b3(n, 0)
             b3(n, 1)
             store_xk(n)
+            if i == 0:
+                load_table(bv, wv_b, 1024, 4096)
+                load_table(bt, bflat, 1024, 4096)
+                load_table(bk, wk_b, 1536, 4096)
+            if i == 1:
+                load_v(2)
             mk(n, 0, VE)
             mk(n, 1, VE)
             token(n)
@@ -625,14 +613,13 @@ def tile_tttwrapper_pa_kernel(
             e2b(i, 0)
             b1(a, 1)
 
-        sq(12, 0)
+        sdt(12, 0)
         dfa(12, 1)
         pe(13, "pv", "pk")
-        c3(15)
-        ngm(12, 1)
         e2a(12, 1)
         e2b(12, 1)
-        sq(12, 1)
+        sdt(12, 1)
+        c3(15)
         b2(15, 0)
         b2(15, 1)
         b3(15, 0)
@@ -643,71 +630,57 @@ def tile_tttwrapper_pa_kernel(
         token(15)
         d2(15, 0, GP)
         d2(15, 1, GP)
-        radd(12, 0)
         dfa(13, 0)
-        pe(14, "pv")
-        rinv(12, 0)
-        ngm(13, 0)
         e2a(13, 0)
         e2b(13, 0)
-        sq(13, 0)
-        radd(12, 1)
+        sdt(13, 0)
+        pe(14, "pv")
+        rat(12, 0)
+        rat(12, 1)
+        dfa(13, 1)
+        e2a(13, 1)
+        e2b(13, 1)
+        sdt(13, 1)
+        pe(15, "pv", "pk")
         f1(12, 0)
         f2(12, 0, GP)
-        rinv(12, 1)
-        dfa(13, 1)
-        pe(15, "pv", "pk")
         f1(12, 1)
         f2(12, 1, GP)
         store_xv(12)
-        ngm(13, 1)
-        e2a(13, 1)
-        e2b(13, 1)
-        sq(13, 1)
-        radd(13, 0)
         dfa(14, 0)
-        rinv(13, 0)
-        ngm(14, 0)
         e2a(14, 0)
         e2b(14, 0)
-        sq(14, 0)
-        f1(13, 0)
-        f2(13, 0, GP)
-        radd(13, 1)
+        sdt(14, 0)
+        rat(13, 0)
         dfa(14, 1)
-        rinv(13, 1)
-        ngm(14, 1)
         e2a(14, 1)
         e2b(14, 1)
-        sq(14, 1)
+        sdt(14, 1)
+        f1(13, 0)
+        f2(13, 0, GP)
+        rat(13, 1)
         f1(13, 1)
         f2(13, 1, GP)
         store_xv(13)
-        radd(14, 0)
         dfa(15, 0)
-        rinv(14, 0)
-        ngm(15, 0)
         e2(15, 0)
-        sq(15, 0)
+        sdt(15, 0)
+        rat(14, 0)
         f1(14, 0)
         f2(14, 0, GP)
         store_xv_half(14, 0)
-        radd(14, 1)
-        rinv(14, 1)
+        dfa(15, 1)
+        e2(15, 1)
+        sdt(15, 1)
+        uu(15, 0)
+        rat(14, 1)
+        rat(15, 0)
         f1(14, 1)
         f2(14, 1, GP)
         store_xv_half(14, 1)
-        dfa(15, 1)
-        radd(15, 0)
-        ngm(15, 1)
-        uu(15, 0)
-        e2(15, 1)
-        sq(15, 1)
-        rinv(15, 0)
         uu(15, 1)
         fin(15, 0)
         store_xv_half(15, 0)
-        radd(15, 1)
-        rinv(15, 1)
+        rat(15, 1)
         fin(15, 1)
         store_xv_half(15, 1)

@@ -75,12 +75,11 @@ def tile_tttwrapper_pa_kernel(
         bk = const.tile([P, 4096], BF16, name="bk", tag="bk")
         bv = const.tile([P, 4096], BF16, name="bv", tag="bv")
         bt = const.tile([P, 4096], BF16, name="bt", tag="bt")
-        wrow = const.tile([P, 4096], BF16, name="wrow", tag="wrow")
+        w8 = const.tile([P, 512], BF16, name="w8", tag="w8")
         fc = const.tile([P, 512], BF16, name="fc", tag="fc")
         fc2 = const.tile([P, 512], BF16, name="fc2", tag="fc2")
         eps = const.tile([P, 4], F32, name="eps", tag="eps")
         scr = const.tile([P, 1], F32, name="scr", tag="scr")
-        ones = const.tile([P, P], BF16, name="ones", tag="ones")
         ident = const.tile([P, P], BF16, name="ident", tag="ident")
         tbl = psum.tile([P, 1024], BF16, name="tbl", tag="tbl", bufs=1)
 
@@ -112,10 +111,9 @@ def tile_tttwrapper_pa_kernel(
             load_scales(vsc[c % WBUF], wv_w_scales, slice(512 * c, 512 * c + 512))
             load_codes(vc, wv_w_words, slice(1024 * c, 1024 * c + 1024))
 
-        nc.gpsimd.memset(wrow[:].bitcast(F32), 0.0)
+        nc.gpsimd.memset(w8[:].bitcast(F32), 0.0)
         make_identity(nc, ident[:])
         nc.vector.memset(hsb[0][:].bitcast(I32), 0)
-        nc.vector.memset(ones[:], 1.0)
         nc.vector.memset(ksc[0][:].bitcast(I32), 0)
         nc.vector.memset(eps[:, E24 : E24 + 1], 1e-24)
         nc.vector.memset(eps[:, NE24 : NE24 + 1], -1e-24)
@@ -128,9 +126,9 @@ def tile_tttwrapper_pa_kernel(
         nc.sync.dma_start(
             out=fc[:].rearrange("p (t n) -> p t n", t=2), in_=freqs_cis.rearrange("(t p) j e -> p t (j e)", p=P)
         )
+        nc.sync.dma_start(out=w8[0:8, :], in_=wflat.rearrange("(c n) -> c n", c=8))
         load_codes(hcb[0], hidden_states_words, slice(0, 512))
         load_scales(hsb[0], hidden_states_scales, slice(0, 256))
-        nc.sync.dma_start(out=wrow[0:1, :], in_=wflat.rearrange("(o n) -> o n", o=1))
         load_codes(kc0, wk_w_words, slice(0, 1024))
         load_scales(ksc[0], wk_w_scales, slice(0, 512))
         load_table(bk, wk_b, 0, 512)
@@ -155,7 +153,6 @@ def tile_tttwrapper_pa_kernel(
         nc.vector.memset(vsc[2][:].bitcast(I32), 0)
 
         nc.tensor.matmul(out=tbl[:, 0:512], lhsT=ident[:], rhs=fc[:], start=True, stop=True)
-        nc.tensor.matmul(out=tbl[:, 512:1024], lhsT=ident[:], rhs=fc2[:], start=True, stop=True)
 
         twt = {}
 
@@ -165,8 +162,8 @@ def tile_tttwrapper_pa_kernel(
                 c = 2 * pair + u
                 nc.tensor.matmul(
                     out=tl[:, 512 * u : 512 * u + 512],
-                    lhsT=ones[:],
-                    rhs=wrow[:, 512 * c : 512 * c + 512],
+                    lhsT=ident[:, c : c + 1].to_broadcast([P, P]),
+                    rhs=w8[:],
                     start=True,
                     stop=True,
                 )
@@ -175,6 +172,7 @@ def tile_tttwrapper_pa_kernel(
         put_w(0)
         put_w(1)
         put_w(2)
+        nc.tensor.matmul(out=tbl[:, 512:1024], lhsT=ident[:], rhs=fc2[:], start=True, stop=True)
 
         SH4 = [P, 2, 128, 2]
         SH3 = [P, 128, 2]

@@ -25,6 +25,7 @@ E24 = 0
 NE24 = 1
 E30 = 2
 E8 = 3
+E8S = 4
 
 
 def tile_tttwrapper_pa_kernel(
@@ -78,7 +79,7 @@ def tile_tttwrapper_pa_kernel(
         w8 = const.tile([P, 512], BF16, name="w8", tag="w8")
         fc = const.tile([P, 512], BF16, name="fc", tag="fc")
         fc2 = const.tile([P, 512], BF16, name="fc2", tag="fc2")
-        eps = const.tile([P, 4], F32, name="eps", tag="eps")
+        eps = const.tile([P, 5], F32, name="eps", tag="eps")
         scr = const.tile([P, 1], F32, name="scr", tag="scr")
         ident = const.tile([P, P], BF16, name="ident", tag="ident")
         tbl = psum.tile([P, 1024], BF16, name="tbl", tag="tbl", bufs=1)
@@ -119,6 +120,7 @@ def tile_tttwrapper_pa_kernel(
         nc.vector.memset(eps[:, NE24 : NE24 + 1], -1e-24)
         nc.vector.memset(eps[:, E30 : E30 + 1], 1e-30)
         nc.vector.memset(eps[:, E8 : E8 + 1], 1e-8)
+        nc.vector.memset(eps[:, E8S : E8S + 1], 256.0e-8)
         nc.scalar.activation(out=scr[:], in_=eps[:, E8 : E8 + 1], func=ACT.Sqrt)
 
         kc0 = wpool.tile([P, G, 1024], U8, name="kc0", tag="kc", align_bytes=64)
@@ -362,6 +364,45 @@ def tile_tttwrapper_pa_kernel(
                 )
             negm = stile(s, "negm")
             nc.scalar.activation(out=negm[:, 2 * t : 2 * t + 2], in_=sm[:, 2 * t : 2 * t + 2], func=ACT.Identity, scale=-1.0 / 256.0)
+
+        def dfn(s, t):
+            pp = wtile(s, "pp", 4)
+            nsm = stile(s, "nsm")
+            for h in range(2):
+                nc.vector.scalar_tensor_tensor(
+                    out=pp[:, t, hsl(h)],
+                    in0=st[s]["pv"][t][:, hsl(h)],
+                    scalar=-1.0,
+                    in1=st[s]["mm"][:, t, hsl(h)],
+                    op0=ALU.mult,
+                    op1=ALU.add,
+                    accum_out=col(nsm, 2 * t + h),
+                )
+
+        def e2n(s, t):
+            pp = st[s]["pp"]
+            for h in range(2):
+                nc.scalar.activation(
+                    out=pp[:, t, hsl(h)],
+                    in_=pp[:, t, hsl(h)],
+                    func=ACT.Identity,
+                    bias=col(st[s]["nsm"], 2 * t + h),
+                    scale=-256.0,
+                )
+
+        def sdn(s, t):
+            sdv = stile(s, "sdv")
+            nc.scalar.activation(
+                out=sdv[:, 2 * t : 2 * t + 2],
+                in_=st[s]["ssd"][:, 2 * t : 2 * t + 2],
+                func=ACT.Sqrt,
+                bias=col(eps, E30),
+                scale=1.0 / (255.0 * 65536.0),
+            )
+            rca = stile(s, "rca")
+            nc.scalar.activation(
+                out=rca[:, 2 * t : 2 * t + 2], in_=sdv[:, 2 * t : 2 * t + 2], func=ACT.Identity, bias=col(eps, E8S), scale=256.0
+            )
 
         def sdt(s, t):
             sdv = stile(s, "sdv")
@@ -612,11 +653,11 @@ def tile_tttwrapper_pa_kernel(
             b1(a, 1)
 
         sdt(12, 0)
-        dfa(12, 1)
+        dfn(12, 1)
         pe(13, "pv", "pk")
-        e2a(12, 1)
+        e2n(12, 1)
         e2b(12, 1)
-        sdt(12, 1)
+        sdn(12, 1)
         c3(15)
         b2(15, 0)
         b2(15, 1)
@@ -628,34 +669,34 @@ def tile_tttwrapper_pa_kernel(
         token(15)
         d2(15, 0, GP)
         d2(15, 1, GP)
-        dfa(13, 0)
-        e2a(13, 0)
+        dfn(13, 0)
+        e2n(13, 0)
         e2b(13, 0)
-        sdt(13, 0)
+        sdn(13, 0)
         pe(14, "pv")
+        dfn(13, 1)
+        e2n(13, 1)
+        e2b(13, 1)
+        sdn(13, 1)
+        pe(15, "pv", "pk")
         rat(12, 0)
         rat(12, 1)
-        dfa(13, 1)
-        e2a(13, 1)
-        e2b(13, 1)
-        sdt(13, 1)
-        pe(15, "pv", "pk")
         f1(12, 0)
         f2(12, 0, GP)
         f1(12, 1)
         f2(12, 1, GP)
         store_xv(12)
-        dfa(14, 0)
-        e2a(14, 0)
+        dfn(14, 0)
+        e2n(14, 0)
         e2b(14, 0)
-        sdt(14, 0)
+        sdn(14, 0)
         rat(13, 0)
-        dfa(14, 1)
-        e2a(14, 1)
-        e2b(14, 1)
-        sdt(14, 1)
         f1(13, 0)
         f2(13, 0, GP)
+        dfn(14, 1)
+        e2n(14, 1)
+        e2b(14, 1)
+        sdn(14, 1)
         rat(13, 1)
         f1(13, 1)
         f2(13, 1, GP)
@@ -672,11 +713,11 @@ def tile_tttwrapper_pa_kernel(
         sdt(15, 1)
         uu(15, 0)
         rat(14, 1)
-        rat(15, 0)
         f1(14, 1)
-        f2(14, 1, GP)
-        store_xv_half(14, 1)
+        rat(15, 0)
         uu(15, 1)
+        f2(14, 1, VE)
+        store_xv_half(14, 1)
         fin(15, 0)
         store_xv_half(15, 0)
         rat(15, 1)

@@ -145,9 +145,9 @@ def tile_tttwrapper_pa_kernel(
         load_codes(hcb[1], hidden_states_words, slice(512, 1024))
         nc.vector.memset(ksc[1][:].bitcast(I32), 0)
         load_k(1)
-        load_table(bk, wk_b, 512, 1024)
-        load_table(bv, wv_b, 0, 512)
-        load_table(bt, bflat, 0, 512)
+        load_table(bk, wk_b, 512, 1536)
+        load_table(bv, wv_b, 0, 1024)
+        load_table(bt, bflat, 0, 1024)
         nc.vector.memset(vsc[0][:].bitcast(I32), 0)
         load_v(0)
         nc.vector.memset(ksc[2][:].bitcast(I32), 0)
@@ -558,9 +558,6 @@ def tile_tttwrapper_pa_kernel(
         b3(0, 1)
         store_xk(0)
         load_k(2)
-        load_table(bv, wv_b, 512, 1024)
-        load_table(bt, bflat, 512, 1024)
-        load_table(bk, wk_b, 1024, 1536)
         pe(2, "pk")
         a1(2, 0)
         c1(2, 0)

from contextlib import ExitStack

import concourse.mybir as mybir
from concourse.masks import make_identity

F32 = mybir.dt.float32
BF16 = mybir.dt.bfloat16
U8 = mybir.dt.uint8
I32 = mybir.dt.int32
FP4 = mybir.dt.float4_e2m1fn_x4
ACT = mybir.ActivationFunctionType
ALU = mybir.AluOpType

FLOPS = 2 * 512 * 4096 * 8192

P = 128
G = 8
NCH = 8
NSUB = 16
WBUF = 3
LEAD = 3
NXB = LEAD + 2

E24 = 0
NE24 = 1
E30 = 2
E8 = 3
E8S = 4


def tile_tttwrapper_pa_kernel(
    tc,
    hidden_states_words,
    hidden_states_scales,
    freqs_cis,
    wk_w_words,
    wk_w_scales,
    wk_b,
    wv_w_words,
    wv_w_scales,
    wv_b,
    ttt_norm_weight,
    ttt_norm_bias,
    out_0,
    out_1,
):
    nc = tc.nc
    o0 = out_0.rearrange("b l h d -> (b l) (h d)")
    o1 = out_1.rearrange("b l h d -> (b l) (h d)")
    wflat = ttt_norm_weight.rearrange("h d -> (h d)")
    bflat = ttt_norm_bias.rearrange("h d -> (h d)")

    with ExitStack() as ctx:
        ctx.enter_context(tc.manual_schedule())
        const = ctx.enter_context(tc.tile_pool(name="const", bufs=1))
        wpool = ctx.enter_context(tc.tile_pool(name="wpool", bufs=WBUF))
        work = ctx.enter_context(tc.tile_pool(name="work", bufs=2))
        small = ctx.enter_context(tc.tile_pool(name="small", bufs=3))
        psum = ctx.enter_context(tc.psum_pool(name="psum", bufs=2))

        hcb = []
        for r in range(2):
            hc_t = const.tile([P, G, 512], U8, name="hc%d" % r, tag="hc%d" % r, align_bytes=64)
            hcb.append(hc_t)
        hsb = []
        for r in range(2):
            hs_t = const.tile([P, G, 256], U8, name="hs%d" % r, tag="hs%d" % r, align_bytes=64)
            hsb.append(hs_t)
        ksc = []
        vsc = []
        for r in range(WBUF):
            ks_t = const.tile([P, G, 512], U8, name="ksc%d" % r, tag="ksc%d" % r, align_bytes=64)
            vs_t = const.tile([P, G, 512], U8, name="vsc%d" % r, tag="vsc%d" % r, align_bytes=64)
            ksc.append(ks_t)
            vsc.append(vs_t)
        bk = const.tile([P, 4096], BF16, name="bk", tag="bk")
        bv = const.tile([P, 4096], BF16, name="bv", tag="bv")
        bt = const.tile([P, 4096], BF16, name="bt", tag="bt")
        w8 = const.tile([P, 512], BF16, name="w8", tag="w8")
        fc = const.tile([P, 512], BF16, name="fc", tag="fc")
        fc2 = const.tile([P, 512], BF16, name="fc2", tag="fc2")
        eps = const.tile([P, 5], F32, name="eps", tag="eps")
        scr = const.tile([P, 1], F32, name="scr", tag="scr")
        ident = const.tile([P, P], BF16, name="ident", tag="ident")
        tbl = psum.tile([P, 1024], BF16, name="tbl", tag="tbl", bufs=1)

        def load_scales(planes, src, cols):
            for q in range(4):
                nc.sync.dma_start(
                    out=planes[32 * q : 32 * q + 4, :, :].bitcast(I32),
                    in_=src[:, 4 * q : 4 * q + 4, cols].rearrange("g r n -> r g n").bitcast(I32),
                )

        def load_codes(dst, src, cols):
            nc.sync.dma_start(out=dst[:].bitcast(I32), in_=src[:, :, cols].rearrange("g p n -> p g n").bitcast(I32))

        def load_table(dst, src, lo, hi):
            nc.sync.dma_start(out=dst[:, lo:hi], in_=src[lo:hi].partition_broadcast(P))

        kcodes = {}
        vcodes = {}

        def load_k(c):
            kc = wpool.tile([P, G, 1024], U8, name="kc%d" % c, tag="kc", align_bytes=64)
            kcodes[c] = kc
            load_scales(ksc[c % WBUF], wk_w_scales, slice(512 * c, 512 * c + 512))
            load_codes(kc, wk_w_words, slice(1024 * c, 1024 * c + 1024))

        def load_v(c):
            vc = wpool.tile([P, G, 1024], U8, name="vc%d" % c, tag="vc", align_bytes=64)
            vcodes[c] = vc
            load_scales(vsc[c % WBUF], wv_w_scales, slice(512 * c, 512 * c + 512))
            load_codes(vc, wv_w_words, slice(1024 * c, 1024 * c + 1024))

        nc.gpsimd.memset(w8[:].bitcast(F32), 0.0)
        make_identity(nc, ident[:])
        nc.vector.memset(hsb[0][:].bitcast(I32), 0)
        nc.vector.memset(ksc[0][:].bitcast(I32), 0)
        nc.vector.memset(eps[:, E24 : E24 + 1], 1e-24)
        nc.vector.memset(eps[:, NE24 : NE24 + 1], -1e-24)
        nc.vector.memset(eps[:, E30 : E30 + 1], 1e-30)
        nc.vector.memset(eps[:, E8 : E8 + 1], 1e-8)
        nc.vector.memset(eps[:, E8S : E8S + 1], 256.0e-8)
        nc.scalar.activation(out=scr[:], in_=eps[:, E8 : E8 + 1], func=ACT.Sqrt)

        kc0 = wpool.tile([P, G, 1024], U8, name="kc0", tag="kc", align_bytes=64)
        kcodes[0] = kc0
        nc.sync.dma_start(
            out=fc[:].rearrange("p (t n) -> p t n", t=2), in_=freqs_cis.rearrange("(t p) j e -> p t (j e)", p=P)
        )
        nc.sync.dma_start(out=w8[0:8, :], in_=wflat.rearrange("(c n) -> c n", c=8))
        load_codes(hcb[0], hidden_states_words, slice(0, 512))
        load_scales(hsb[0], hidden_states_scales, slice(0, 256))
        load_codes(kc0, wk_w_words, slice(0, 1024))
        load_scales(ksc[0], wk_w_scales, slice(0, 512))
        load_table(bk, wk_b, 0, 512)

        fcv = fc[:].rearrange("p (n e) -> p n e", e=2)
        fc2v = fc2[:].rearrange("p (n e) -> p n e", e=2)
        nc.vector.tensor_scalar_mul(out=fc2v[:, :, 0:1], in0=fcv[:, :, 1:2], scalar1=-1.0)
        nc.vector.tensor_copy(out=fc2v[:, :, 1:2], in_=fcv[:, :, 0:1])

        nc.vector.memset(hsb[1][:].bitcast(I32), 0)
        load_scales(hsb[1], hidden_states_scales, slice(256, 512))
        load_codes(hcb[1], hidden_states_words, slice(512, 1024))
        nc.vector.memset(ksc[1][:].bitcast(I32), 0)
        load_k(1)
        load_table(bk, wk_b, 512, 1536)
        load_table(bv, wv_b, 0, 1024)
        load_table(bt, bflat, 0, 1024)
        nc.vector.memset(vsc[0][:].bitcast(I32), 0)
        load_v(0)
        nc.vector.memset(ksc[2][:].bitcast(I32), 0)
        nc.vector.memset(vsc[1][:].bitcast(I32), 0)
        nc.vector.memset(vsc[2][:].bitcast(I32), 0)

        nc.tensor.matmul(out=tbl[:, 0:512], lhsT=ident[:], rhs=fc[:], start=True, stop=True)

        twt = {}

        def put_w(pair):
            tl = psum.tile([P, 1024], BF16, name="tw_%d" % pair, tag="tw%d" % (pair % 3), bufs=1)
            for u in range(2):
                c = 2 * pair + u
                nc.tensor.matmul(
                    out=tl[:, 512 * u : 512 * u + 512],
                    lhsT=ident[:, c : c + 1].to_broadcast([P, P]),
                    rhs=w8[:],
                    start=True,
                    stop=True,
                )
                twt[c] = tl[:, 512 * u : 512 * u + 512]

        put_w(0)
        put_w(1)
        put_w(2)
        nc.tensor.matmul(out=tbl[:, 512:1024], lhsT=ident[:], rhs=fc2[:], start=True, stop=True)

        SH4 = [P, 2, 128, 2]
        SH3 = [P, 128, 2]

        def v4(ap):
            return ap.rearrange("p (h j e) -> p h j e", h=2, j=128, e=2)

        def v3(ap):
            return ap.rearrange("p (j e) -> p j e", e=2)

        st = {}
        for s in range(NSUB):
            st[s] = {}

        def ok(s):
            return 0 <= s < NSUB

        def pe(s, kind, tag=None):
            if not ok(s):
                return
            c, b = divmod(s, 2)
            codes = (kcodes if kind == "pk" else vcodes)[c]
            planes = (ksc if kind == "pk" else vsc)[c % WBUF]
            res = []
            for t in range(2):
                acc = psum.tile([P, 512], F32, name="%s_%d_%d" % (kind, s, t), tag=(tag or kind), bufs=2)
                for g in range(G):
                    nc.tensor.matmul_mx(
                        out=acc[:],
                        lhsT=hcb[b][:, g, 256 * t : 256 * t + 256].bitcast(FP4),
                        lhsT_scale=hsb[b][:, g, 128 * t : 128 * t + 128],
                        rhs=codes[:, g, :].bitcast(FP4),
                        rhs_scale=planes[:, g, :],
                        start=(g == 0),
                        stop=(g == G - 1),
                    )
                res.append(acc)
            st[s][kind] = res

        def cols(s):
            c = s // 2
            return slice(512 * c, 512 * c + 512)

        def rows(s, t):
            r0 = 256 * (s % 2) + 128 * t
            return slice(r0, r0 + 128)

        def rows2(s):
            b = s % 2
            return slice(256 * b, 256 * b + 256)

        def wtile(s, nm, bufs):
            if nm not in st[s]:
                tl = work.tile([P, 2, 512], F32, name="%s%d" % (nm, s), tag=nm, bufs=bufs)
                st[s][nm] = tl
            return st[s][nm]

        def stile(s, nm):
            if nm not in st[s]:
                tl = small.tile([P, 4], F32, name="%s%d" % (nm, s), tag=nm, bufs=4)
                st[s][nm] = tl
            return st[s][nm]

        def junk():
            return work.tile([P, 256], F32, name="junk", tag="junk", bufs=4)

        def hsl(h):
            return slice(256 * h, 256 * h + 256)

        def col(tl, k):
            return tl[:, k : k + 1]

        def a1(s, t):
            if not ok(s):
                return
            k0 = wtile(s, "k0", 2)
            nc.vector.tensor_tensor(out=k0[:, t, :], in0=st[s]["pk"][t][:], in1=bk[:, cols(s)], op=ALU.add)

        def c1(s, t):
            if not ok(s):
                return
            ss = stile(s, "ss")
            for h in range(2):
                jk = junk()
                nc.scalar.activation(
                    out=jk[:], in_=st[s]["k0"][:, t, hsl(h)], func=ACT.Square, accum_out=col(ss, 2 * t + h)
                )

        def c2(s):
            if not ok(s):
                return
            r1 = stile(s, "r1")
            nc.scalar.activation(out=r1[:], in_=st[s]["ss"][:], func=ACT.Relu, bias=col(eps, NE24), scale=1.0)
            rcn = stile(s, "rcn")
            nc.scalar.activation(out=rcn[:], in_=r1[:], func=ACT.Sqrt, bias=col(eps, E24), scale=1.0)

        def c3(s):
            if not ok(s):
                return
            rno = stile(s, "rno")
            nc.vector.reciprocal(out=rno[:], in_=st[s]["rcn"][:])

        def b1(s, t):
            if not ok(s):
                return
            t1 = wtile(s, "t1", 2)
            nc.vector.tensor_tensor(
                out=v4(t1[:, t, :]),
                in0=v4(st[s]["k0"][:, t, :])[:, :, :, 0:1].to_broadcast(SH4),
                in1=v3(tbl[:, 256 * t : 256 * t + 256]).unsqueeze(1).to_broadcast(SH4),
                op=ALU.mult,
            )

        def b2(s, t):
            if not ok(s):
                return
            t2 = wtile(s, "t2", 2)
            for h in range(2):
                nc.vector.scalar_tensor_tensor(
                    out=v3(t2[:, t, hsl(h)]),
                    in0=v3(st[s]["k0"][:, t, hsl(h)])[:, :, 1:2].to_broadcast(SH3),
                    scalar=col(st[s]["rno"], 2 * t + h),
                    in1=v3(tbl[:, 512 + 256 * t : 512 + 256 * t + 256]),
                    op0=ALU.mult,
                    op1=ALU.mult,
                )

        def b3(s, t):
            if not ok(s):
                return
            xk = wtile(s, "xk", 3)
            for h in range(2):
                nc.vector.scalar_tensor_tensor(
                    out=xk[:, t, hsl(h)],
                    in0=st[s]["t1"][:, t, hsl(h)],
                    scalar=col(st[s]["rno"], 2 * t + h),
                    in1=st[s]["t2"][:, t, hsl(h)],
                    op0=ALU.mult,
                    op1=ALU.add,
                )

        def store_xk(s):
            if not ok(s):
                return
            nc.sync.dma_start(out=o0[rows2(s), cols(s)].rearrange("(t p) n -> p t n", p=P), in_=st[s]["xk"][:])

        def mk(s, t, eng):
            if not ok(s):
                return
            mm = wtile(s, "mm", LEAD + 1)
            eng.tensor_tensor(out=mm[:, t, :], in0=st[s]["xk"][:, t, :], in1=bv[:, cols(s)], op=ALU.subtract)

        def token(s):
            if not ok(s):
                return
            tok = work.tile([P, 1], F32, name="tok%d" % s, tag="xa%d" % (s % NXB), bufs=1)
            nc.vector.memset(tok[:], 0.0)

        def d2(s, t, eng):
            if not ok(s):
                return
            if t == 0:
                xb = work.tile([P, 512], F32, name="xb0_%d" % s, tag="xa%d" % (s % NXB), bufs=1)
            else:
                xb = work.tile([P, 512], F32, name="xb1_%d" % s, tag="xc", bufs=NXB)
            st[s]["xb%d" % t] = xb
            eng.tensor_tensor(out=xb[:], in0=st[s]["xk"][:, t, :], in1=bt[:, cols(s)], op=ALU.add)

        def df(s, t):
            if not ok(s):
                return
            pp = wtile(s, "pp", 4)
            nc.vector.tensor_tensor(out=pp[:, t, :], in0=st[s]["pv"][t][:], in1=st[s]["mm"][:, t, :], op=ALU.subtract)

        def dfa(s, t):
            pp = wtile(s, "pp", 4)
            sm = stile(s, "sm")
            for h in range(2):
                nc.vector.scalar_tensor_tensor(
                    out=pp[:, t, hsl(h)],
                    in0=st[s]["pv"][t][:, hsl(h)],
                    scalar=1.0,
                    in1=st[s]["mm"][:, t, hsl(h)],
                    op0=ALU.mult,
                    op1=ALU.subtract,
                    accum_out=col(sm, 2 * t + h),
                )
            negm = stile(s, "negm")
            nc.scalar.activation(out=negm[:, 2 * t : 2 * t + 2], in_=sm[:, 2 * t : 2 * t + 2], func=ACT.Identity, scale=-1.0 / 256.0)

        def dfn(s, t):
            pp = wtile(s, "pp", 4)
            nsm = stile(s, "nsm")
            for h in range(2):
                nc.vector.scalar_tensor_tensor(
                    out=pp[:, t, hsl(h)],
                    in0=st[s]["pv"][t][:, hsl(h)],
                    scalar=-1.0,
                    in1=st[s]["mm"][:, t, hsl(h)],
                    op0=ALU.mult,
                    op1=ALU.add,
                    accum_out=col(nsm, 2 * t + h),
                )

        def e2n(s, t):
            pp = st[s]["pp"]
            for h in range(2):
                nc.scalar.activation(
                    out=pp[:, t, hsl(h)],
                    in_=pp[:, t, hsl(h)],
                    func=ACT.Identity,
                    bias=col(st[s]["nsm"], 2 * t + h),
                    scale=-256.0,
                )

        def sdn(s, t):
            sdv = stile(s, "sdv")
            nc.scalar.activation(
                out=sdv[:, 2 * t : 2 * t + 2],
                in_=st[s]["ssd"][:, 2 * t : 2 * t + 2],
                func=ACT.Sqrt,
                bias=col(eps, E30),
                scale=1.0 / (255.0 * 65536.0),
            )
            rca = stile(s, "rca")
            nc.scalar.activation(
                out=rca[:, 2 * t : 2 * t + 2], in_=sdv[:, 2 * t : 2 * t + 2], func=ACT.Identity, bias=col(eps, E8S), scale=256.0
            )

        def sdt(s, t):
            sdv = stile(s, "sdv")
            nc.scalar.activation(
                out=sdv[:, 2 * t : 2 * t + 2], in_=st[s]["ssd"][:, 2 * t : 2 * t + 2], func=ACT.Sqrt, bias=col(eps, E30), scale=1.0 / 255.0
            )
            rca = stile(s, "rca")
            nc.scalar.activation(out=rca[:, 2 * t : 2 * t + 2], in_=sdv[:, 2 * t : 2 * t + 2], func=ACT.Identity, bias=col(eps, E8), scale=1.0)

        def rat(s, t):
            rca = stile(s, "rca")
            rao = stile(s, "rao")
            nc.vector.reciprocal(out=rao[:, 2 * t : 2 * t + 2], in_=rca[:, 2 * t : 2 * t + 2])

        def e1(s, t):
            if not ok(s):
                return
            negm = stile(s, "negm")
            for h in range(2):
                jk = junk()
                nc.scalar.activation(
                    out=jk[:],
                    in_=st[s]["pp"][:, t, hsl(h)],
                    func=ACT.Identity,
                    scale=-1.0 / 256.0,
                    accum_out=col(negm, 2 * t + h),
                )

        def e2a(s, t):
            if not ok(s):
                return
            pp = st[s]["pp"]
            for h in range(2):
                nc.scalar.activation(
                    out=pp[:, t, hsl(h)],
                    in_=pp[:, t, hsl(h)],
                    func=ACT.Identity,
                    bias=col(st[s]["negm"], 2 * t + h),
                    scale=1.0,
                )

        def e2b(s, t):
            if not ok(s):
                return
            ssd = stile(s, "ssd")
            for h in range(2):
                jk = junk()
                nc.scalar.activation(
                    out=jk[:], in_=st[s]["pp"][:, t, hsl(h)], func=ACT.Square, accum_out=col(ssd, 2 * t + h)
                )

        def e2(s, t):
            ssd = stile(s, "ssd")
            for h in range(2):
                jk = junk()
                nc.scalar.activation(
                    out=jk[:],
                    in_=st[s]["pp"][:, t, hsl(h)],
                    func=ACT.Square,
                    bias=col(st[s]["negm"], 2 * t + h),
                    scale=1.0,
                    accum_out=col(ssd, 2 * t + h),
                )

        def sd(s, lo, hi):
            if not ok(s):
                return
            sdv = stile(s, "sdv")
            nc.scalar.activation(
                out=sdv[:, lo:hi], in_=st[s]["ssd"][:, lo:hi], func=ACT.Sqrt, bias=col(eps, E30), scale=1.0 / 255.0
            )
            rca = stile(s, "rca")
            nc.scalar.activation(out=rca[:, lo:hi], in_=sdv[:, lo:hi], func=ACT.Identity, bias=col(eps, E8), scale=1.0)

        def ra(s, lo, hi):
            if not ok(s):
                return
            rao = stile(s, "rao")
            nc.vector.reciprocal(out=rao[:, lo:hi], in_=st[s]["rca"][:, lo:hi])

        def f1(s, t):
            if not ok(s):
                return
            pp = st[s]["pp"]
            for h in range(2):
                nc.vector.scalar_tensor_tensor(
                    out=pp[:, t, hsl(h)],
                    in0=pp[:, t, hsl(h)],
                    scalar=col(st[s]["rao"], 2 * t + h),
                    in1=twt[s // 2][:, hsl(h)],
                    op0=ALU.mult,
                    op1=ALU.mult,
                )

        def f2(s, t, eng):
            if not ok(s):
                return
            pp = st[s]["pp"]
            eng.tensor_tensor(out=pp[:, t, :], in0=pp[:, t, :], in1=st[s]["xb%d" % t][:], op=ALU.add)

        def store_xv(s):
            if not ok(s):
                return
            nc.sync.dma_start(out=o1[rows2(s), cols(s)].rearrange("(t p) n -> p t n", p=P), in_=st[s]["pp"][:])

        def store_xv_half(s, t):
            nc.sync.dma_start(out=o1[rows(s, t), cols(s)], in_=st[s]["pp"][:, t, :])

        def uu(s, t):
            u = wtile(s, "t1u", 1)
            for h in range(2):
                nc.vector.scalar_tensor_tensor(
                    out=u[:, t, hsl(h)],
                    in0=st[s]["pp"][:, t, hsl(h)],
                    scalar=col(st[s]["negm"], 2 * t + h),
                    in1=twt[s // 2][:, hsl(h)],
                    op0=ALU.add,
                    op1=ALU.mult,
                )

        def fin(s, t):
            for h in range(2):
                nc.vector.scalar_tensor_tensor(
                    out=st[s]["pp"][:, t, hsl(h)],
                    in0=st[s]["t1u"][:, t, hsl(h)],
                    scalar=col(st[s]["rao"], 2 * t + h),
                    in1=st[s]["xb%d" % t][:, hsl(h)],
                    op0=ALU.mult,
                    op1=ALU.add,
                )

        GP = nc.gpsimd
        VE = nc.vector

        pe(0, "pk")
        a1(0, 0)
        c1(0, 0)
        b1(0, 0)
        a1(0, 1)
        c1(0, 1)
        c2(0)
        b1(0, 1)
        pe(1, "pk")
        a1(1, 0)
        c1(1, 0)
        c3(0)
        b2(0, 0)
        b2(0, 1)
        a1(1, 1)
        c1(1, 1)
        c2(1)
        b3(0, 0)
        b3(0, 1)
        store_xk(0)
        load_k(2)
        pe(2, "pk")
        a1(2, 0)
        c1(2, 0)
        mk(0, 0, VE)
        mk(0, 1, VE)
        token(0)
        d2(0, 0, GP)
        d2(0, 1, GP)
        b1(1, 0)
        a1(2, 1)
        c1(2, 1)
        c2(2)
        b1(1, 1)
        c3(1)
        b2(1, 0)
        b2(1, 1)
        b3(1, 0)
        b3(1, 1)
        store_xk(1)
        load_v(1)
        load_k(3)
        mk(1, 0, VE)
        mk(1, 1, VE)
        token(1)
        d2(1, 0, GP)
        d2(1, 1, GP)
        b1(2, 0)
        b1(2, 1)

        for i in range(0, NSUB - LEAD):
            a = i + LEAD
            n = a - 1
            j = i - 1
            if a % 2 == 0 and a // 2 + 2 < NCH:
                load_k(a // 2 + 2)
            if i % 2 == 0 and i >= 2 and i // 2 + 2 < NCH:
                load_v(i // 2 + 2)
            if i == 6:
                put_w(3)
            pe(a, "pk")
            df(j, 1)
            pe(i, "pv")
            e1(j, 1)
            e2a(j, 1)
            e2b(j, 1)
            sd(j, 0, 4)
            late = i == 0
            if late:
                a1(a, 0)
                c1(a, 0)
            c3(n)
            b2(n, 0)
            b2(n, 1)
            if late:
                a1(a, 1)
                c1(a, 1)
                c2(a)
            if not late:
                a1(a, 0)
                c1(a, 0)
            b3(n, 0)
            b3(n, 1)
            store_xk(n)
            if i == 0:
                load_table(bv, wv_b, 1024, 4096)
                load_table(bt, bflat, 1024, 4096)
                load_table(bk, wk_b, 1536, 4096)
            if i == 1:
                load_v(2)
            mk(n, 0, VE)
            mk(n, 1, VE)
            token(n)
            d2(n, 0, GP)
            d2(n, 1, GP)
            if not late:
                a1(a, 1)
                c1(a, 1)
                c2(a)
            ra(j, 0, 4)
            f1(j, 0)
            f1(j, 1)
            f2(j, 0, GP)
            f2(j, 1, GP)
            store_xv(j)
            b1(a, 0)
            df(i, 0)
            e1(i, 0)
            e2a(i, 0)
            e2b(i, 0)
            b1(a, 1)

        sdt(12, 0)
        dfn(12, 1)
        pe(13, "pv", "pk")
        e2n(12, 1)
        e2b(12, 1)
        sdn(12, 1)
        c3(15)
        b2(15, 0)
        b2(15, 1)
        b3(15, 0)
        b3(15, 1)
        store_xk(15)
        mk(15, 0, VE)
        mk(15, 1, VE)
        token(15)
        d2(15, 0, GP)
        d2(15, 1, GP)
        dfn(13, 0)
        e2n(13, 0)
        e2b(13, 0)
        sdn(13, 0)
        pe(14, "pv")
        dfn(13, 1)
        e2n(13, 1)
        e2b(13, 1)
        sdn(13, 1)
        pe(15, "pv", "pk")
        rat(12, 0)
        rat(12, 1)
        f1(12, 0)
        f2(12, 0, GP)
        f1(12, 1)
        f2(12, 1, GP)
        store_xv(12)
        dfn(14, 0)
        e2n(14, 0)
        e2b(14, 0)
        sdn(14, 0)
        rat(13, 0)
        f1(13, 0)
        f2(13, 0, GP)
        dfn(14, 1)
        e2n(14, 1)
        e2b(14, 1)
        sdn(14, 1)
        rat(13, 1)
        f1(13, 1)
        f2(13, 1, GP)
        store_xv(13)
        dfa(15, 0)
        e2(15, 0)
        sdt(15, 0)
        rat(14, 0)
        f1(14, 0)
        f2(14, 0, GP)
        store_xv_half(14, 0)
        dfa(15, 1)
        e2(15, 1)
        sdt(15, 1)
        uu(15, 0)
        rat(14, 1)
        f1(14, 1)
        rat(15, 0)
        uu(15, 1)
        f2(14, 1, VE)
        store_xv_half(14, 1)
        fin(15, 0)
        store_xv_half(15, 0)
        rat(15, 1)
        fin(15, 1)
        store_xv_half(15, 1)
